import numpy as np
import ml_dtypes


def mxq(x, axis, fmt="e4m3"):
    dtype, down = {"e4m3": (ml_dtypes.float8_e4m3fn, 7), "e5m2": (ml_dtypes.float8_e5m2, 14)}[fmt]
    v = np.moveaxis(np.asarray(x, np.float32).astype(ml_dtypes.bfloat16).astype(np.float64), axis, -1)
    blocks = v.reshape(v.shape[:-1] + (-1, 32))
    amax = np.abs(blocks).max(-1, keepdims=True)
    byte = np.maximum(np.where(amax > 0, np.frexp(amax)[1] - 1 + 127, 0) - down, 1)
    scale = np.exp2(byte - 127.0)
    codes = (blocks / scale).astype(np.float32).astype(dtype).astype(np.float64)
    return np.moveaxis((codes * scale).reshape(v.shape), -1, axis)


WIDE = False


def mx_kscale(k):
    if not WIDE:
        return np.ones(k)
    levels = np.array([10, -10, 5, -5, 0])
    if k % 512:
        return np.exp2(np.random.permutation(np.resize(levels, k // 32))).repeat(32)
    a = np.empty((k // 512, 16))
    for p in range(k // 512):
        a[p, :8] = np.random.permutation(np.resize(levels, 8))
        for g in range(8):
            far = levels[np.abs(levels - a[p, g]) >= 10]
            a[p, g + 8] = far[np.random.randint(len(far))]
    return np.exp2(a.ravel()).repeat(32)


BF16 = ml_dtypes.bfloat16


def bf(x):
    return np.asarray(x, np.float32).astype(BF16)


def f64(x):
    return np.asarray(x).astype(np.float64)


B, T, C, HQ, HKV, HD = 4, 256, 2048, 16, 4, 128
EPS = 1e-6


def apply_rope(u, cos, sin):
    c = cos[None, :, None, :]
    s = sin[None, :, None, :]
    u1, u2 = u[..., ::2], u[..., 1::2]
    return np.concatenate([u1 * c - u2 * s, u1 * s + u2 * c], axis=-1)


def rmsnorm(u, w):
    return w * (u / np.sqrt(np.mean(u * u, axis=-1, keepdims=True) + EPS))


def draw0():
    s = mx_kscale(C)
    inv_freq = 1.0 / (10000.0 ** (np.arange(0, HD, 2) / HD))
    freqs = np.arange(T)[:, None] * inv_freq[None, :]
    return {"x": bf(np.random.standard_normal((B, T, C)) * s),
            "Wq": bf(np.random.standard_normal((HQ * HD, C)) / np.sqrt(C) / s),
            "bq": bf(np.random.standard_normal(HQ * HD) * 0.3),
            "Wk": bf(np.random.standard_normal((HKV * HD, C)) / np.sqrt(C) / s),
            "bk": bf(np.random.standard_normal(HKV * HD) * 0.3),
            "qn_w": bf(1.0 + 0.1 * np.random.standard_normal(HD)),
            "kn_w": bf(1.0 + 0.1 * np.random.standard_normal(HD)),
            "cos": bf(np.cos(freqs)),
            "sin": bf(np.sin(freqs))}


def core(x, Wq, bq, Wk, bk, qn_w, kn_w, cos, sin):
    xq = mxq(f64(x).reshape(B * T, C), 1, "e4m3")
    q = ((xq @ mxq(f64(Wq), 1, "e4m3").T) + f64(bq)).reshape(B, T, HQ, HD)
    k = ((xq @ mxq(f64(Wk), 1, "e4m3").T) + f64(bk)).reshape(B, T, HKV, HD)
    q = rmsnorm(apply_rope(q, f64(cos), f64(sin)), f64(qn_w))
    k = rmsnorm(apply_rope(k, f64(cos), f64(sin)), f64(kn_w))
    return q, k


def e4m3fn_bytes(y):
    return np.clip(np.asarray(y, np.float64), -448.0, 448.0).astype(np.float32).astype(ml_dtypes.float8_e4m3fn).view(np.uint8)


def e4m3fn_values(b):
    return np.asarray(b, np.uint8).view(ml_dtypes.float8_e4m3fn).astype(np.float64)


def setup_inputs():
    d = draw0()
    x0 = np.asarray(d['Wq']).astype(np.float64)
    s = (np.max(np.abs(x0), axis=(0,), keepdims=True) / 448.0).astype(np.float32)
    out = {}
    for k, v in d.items():
        if k == 'Wq':
            out['Wq_bytes'] = e4m3fn_bytes(x0 / s.astype(np.float64))
            out['Wq_scale'] = s
        else:
            out[k] = v
    return out


def reference(x, Wq_bytes, Wq_scale, bq, Wk, bk, qn_w, kn_w, cos, sin):
    return core(x, e4m3fn_values(Wq_bytes) * Wq_scale.astype(np.float64), bq, Wk, bk, qn_w, kn_w, cos, sin)

@@ -1,0 +1,481 @@
+from contextlib import ExitStack
+
+import concourse.mybir as mybir
+from concourse.masks import make_identity
+
+F32 = mybir.dt.float32
+BF16 = mybir.dt.bfloat16
+U32 = mybir.dt.uint32
+U8 = mybir.dt.uint8
+FP8 = mybir.dt.float8_e4m3fn
+FP8X4 = mybir.dt.float8_e4m3fn_x4
+ALU = mybir.AluOpType
+ACT = mybir.ActivationFunctionType
+
+P = 128
+K = 2048
+PASSES = 4
+TOKENS = 1024
+HALF = 512
+EPS = 1e-6
+N_Q_PAIRS = 8
+N_K_PAIRS = 2
+N_PAIRS = N_Q_PAIRS + N_K_PAIRS
+N_UNITS = 2 * N_PAIRS
+V_TAIL = 2
+
+FLOPS = 2 * TOKENS * (2048 + 512) * K
+
+
+def tile_gqaselfattention_pa_kernel(
+    tc, x, Wq_bytes, Wq_scale, bq, Wk, bk, qn_w, kn_w, cos, sin, out_0, out_1
+):
+    nc = tc.nc
+    x_view = x.flatten_outer_dims().rearrange("(n p) k -> n p k", p=P)
+    wq_view = Wq_bytes.rearrange("(j p e) k -> j p e k", p=P, e=2)
+    wk_view = Wk.rearrange("(j p e) k -> j p e k", p=P, e=2)
+    oq_view = out_0.rearrange("b t h d -> (b t) (h d)").rearrange("(n p) c -> p n c", p=P)
+    ok_view = out_1.rearrange("b t h d -> (b t) (h d)").rearrange("(n p) c -> p n c", p=P)
+    order = [0, 1, 8, 2, 3, 4, 9, 5, 6, 7]
+
+    with ExitStack() as ctx:
+        const = ctx.enter_context(tc.tile_pool(name="const", bufs=1))
+        xin = ctx.enter_context(tc.tile_pool(name="xin", bufs=8))
+        xkeep = ctx.enter_context(tc.tile_pool(name="xkeep", bufs=1))
+        bpool = ctx.enter_context(tc.tile_pool(name="bpool", bufs=4))
+        wbpool = ctx.enter_context(tc.tile_pool(name="wbpool", bufs=5))
+        wpool = ctx.enter_context(tc.tile_pool(name="wpool", bufs=3))
+        gpool = ctx.enter_context(tc.tile_pool(name="gpool", bufs=2))
+        tpool = ctx.enter_context(tc.tile_pool(name="tpool", bufs=2))
+        ypool = ctx.enter_context(tc.tile_pool(name="ypool", bufs=3))
+        spool = ctx.enter_context(tc.tile_pool(name="spool", bufs=4))
+        ps_tp = ctx.enter_context(tc.psum_pool(name="ps_tp", bufs=2))
+        ps_mx = ctx.enter_context(tc.psum_pool(name="ps_mx", bufs=4))
+        ps_ot = ctx.enter_context(tc.psum_pool(name="ps_ot", bufs=2))
+
+        cs_bf = const.tile([P, 2, 2, 64], BF16, name="cs_bf")
+        brow_bf = const.tile([P, 256], BF16, name="brow_bf")
+        warm = const.tile([P, 1], F32, name="warm")
+        warm_out = const.tile([P, 1], F32, name="warm_out")
+        ident = const.tile([P, P], F32, name="ident")
+        sc_bc = const.tile([P, K], F32, name="sc_bc")
+        wq_bc = const.tile([P, P], BF16, name="wq_bc")
+        wk_bc = const.tile([P, P], BF16, name="wk_bc")
+        nc.vector.memset(brow_bf[:], 0.0)
+        nc.vector.memset(warm[:], 1.0)
+        make_identity(nc, ident[:])
+
+        x_sb = []
+        for n in range(8):
+            xt = xin.tile([P, K], BF16, name="x_sb", tag="x_sb")
+            x_sb.append(xt)
+        xc = xkeep.tile([P, PASSES, TOKENS], U32, name="xc", align_bytes=64)
+        xs = xkeep.tile([P, PASSES, TOKENS], U8, name="xs", align_bytes=64)
+        xg = []
+        for h in range(2):
+            xgh = xkeep.tile([P, PASSES, HALF, 4], BF16, name="xg%d" % h, align_bytes=64)
+            xg.append(xgh)
+
+        ctx.enter_context(tc.manual_schedule())
+
+        nc.sync.dma_start(out=cs_bf[:, 0, :, :], in_=cos.rearrange("(b p) i -> p b i", p=P))
+        nc.sync.dma_start(out=cs_bf[:, 1, :, :], in_=sin.rearrange("(b p) i -> p b i", p=P))
+        nc.scalar.activation(out=warm_out[:], in_=warm[:], func=ACT.Abs_reciprocal_sqrt)
+
+        wb_of = {}
+        by_of = {}
+        wg_of = {}
+        codes_of = {}
+        acc_of = {}
+        prods_of = {}
+        ots_of = {}
+        ss_of = {}
+        rstd_of = {}
+        y_of = {}
+        late = []
+
+        def load_x(i):
+            nc.sync.dma_start(out=x_sb[i][:], in_=x_view[i])
+
+        def load_w(n):
+            j = order[n]
+            if j >= N_Q_PAIRS:
+                wb = wbpool.tile([P, 2, K], BF16, name="wb", tag="wb")
+                wb_of[n] = wb
+                nc.sync.dma_start(out=wb[:], in_=wk_view[j - N_Q_PAIRS])
+            else:
+                by = bpool.tile([P, 2, K], U8, name="wq_bytes_sb", tag="wq_bytes_sb")
+                by_of[n] = by
+                nc.sync.dma_start(out=by[:], in_=wq_view[j])
+
+        def prod(n, e, lo=0, hi=K):
+            if n not in wb_of:
+                wb = wbpool.tile([P, 2, K], BF16, name="wb", tag="wb")
+                wb_of[n] = wb
+            nc.vector.tensor_tensor(
+                out=wb_of[n][:, e, lo:hi], in0=by_of[n][:, e, lo:hi].bitcast(FP8), in1=sc_bc[:, lo:hi], op=ALU.mult
+            )
+
+        def flush_late():
+            for tp, dst in late:
+                nc.scalar.copy(out=dst, in_=tp[:].rearrange("p g u r -> p g r u"))
+            late.clear()
+
+        def head_bank(where):
+            if where == "mx":
+                bank = ps_mx.tile([P, 2, 2, P], F32, name="mx", tag="mx")
+            elif where == "ot":
+                bank = ps_ot.tile([P, 2, 2, P], F32, name="ot", tag="ot")
+            else:
+                bank = ps_tp.tile([P, 2, 2, P], F32, name="tp", tag="tp")
+            return bank
+
+        def transpose_rows(src_bf, dst_words, defer, where=("tp", "tp")):
+            words = src_bf.bitcast(F32)
+            for gp in range(2):
+                tp = head_bank(where[gp])
+                for g2 in range(2):
+                    g = 2 * gp + g2
+                    for u in range(2):
+                        nc.tensor.transpose(
+                            tp[:, g2, u, :], words[:, 256 * g + u : 256 * (g + 1) : 2], ident[:]
+                        )
+                late.append((tp, dst_words[:, 2 * gp : 2 * gp + 2, :, :]))
+                if not (defer and gp == 1):
+                    flush_late()
+
+        def xt_(i, where):
+            h, tl = divmod(i, 4)
+            transpose_rows(x_sb[i][:], xg[h][:].bitcast(F32)[:, :, tl * P : (tl + 1) * P, :], False, where)
+
+        def qx(h, tp2):
+            for g in range(PASSES):
+                lo = h * HALF + tp2 * 256
+                nc.vector.quantize_mx(
+                    out=xc[:, g, lo : lo + 256].bitcast(FP8X4),
+                    scales=xs[:, g, lo : lo + 256],
+                    in_=xg[h][:, g, tp2 * 256 : (tp2 + 1) * 256, :].rearrange("p n t -> p (n t)"),
+                )
+
+        def bt(m, defer, where=("tp", "tp")):
+            n, e = divmod(m, 2)
+            if e == 0:
+                wg = gpool.tile([P, 2, PASSES, P, 4], BF16, name="wg", tag="wg", align_bytes=64)
+                wg_of[n] = wg
+            transpose_rows(wb_of[n][:, e, :], wg_of[n][:].bitcast(F32)[:, e, :, :, :], defer, where)
+
+        def qw(n):
+            wc = wpool.tile([P, 2 * PASSES * P], U32, name="wc", tag="wc", align_bytes=64)
+            ws = wpool.tile([P, 2 * PASSES * P], U8, name="ws", tag="ws", align_bytes=64)
+            nc.vector.quantize_mx(
+                out=wc[:].bitcast(FP8X4), scales=ws[:], in_=wg_of[n][:].rearrange("p e g r t -> p (e g r t)")
+            )
+            codes_of[n] = (wc, ws)
+
+        cs_f = const.tile([P, 2, 2, 2, 64], F32, name="cs_f")
+        brow_f = const.tile([P, 256], F32, name="brow_f")
+
+        def setup_widen():
+            for hh in range(2):
+                nc.scalar.copy(out=cs_f[:, :, :, hh, :], in_=cs_bf[:])
+
+        def setup_tables():
+            tp_cs = ps_ot.tile([P, 2, 2, P], F32, name="ot", tag="ot")
+            for c in range(2):
+                for b in range(2):
+                    nc.tensor.transpose(
+                        tp_cs[:, c, b, :], cs_f[:, c, b, :, :].rearrange("p h i -> p (h i)"), ident[:]
+                    )
+            for rep in range(2):
+                nc.scalar.copy(out=ctab[:, rep, :], in_=tp_cs[:, 0, :, :].rearrange("p b t -> p (b t)"))
+                nc.scalar.copy(out=stab[:, rep, :], in_=tp_cs[:, 1, :, :].rearrange("p b t -> p (b t)"))
+                nc.scalar.mul(out=ntab[:, rep, :], in_=tp_cs[:, 1, :, :].rearrange("p b t -> p (b t)"), mul=-1.0)
+
+        def setup_bias():
+            nc.scalar.copy(out=brow_f[:], in_=brow_bf[:])
+            tp_b = ps_ot.tile([P, 2, 2, P], F32, name="ot", tag="ot")
+            brow_v = brow_f[:].rearrange("p (c e) -> p e c", e=2)
+            for e in range(2):
+                nc.tensor.transpose(tp_b[:, 0, e, :], brow_v[:, e, :], ident[:])
+            nc.scalar.copy(out=bias_sb[:, :, 0:10], in_=tp_b[:, 0, :, 0:10])
+
+        def setup_gains():
+            for wr, src in ((w_rep_q, wq_bc), (w_rep_k, wk_bc)):
+                for r in range(4):
+                    nc.gpsimd.tensor_copy(out=wr[:, r, :], in_=src[:])
+
+        ctab = const.tile([P, 2, 256], F32, name="ctab")
+        stab = const.tile([P, 2, 256], F32, name="stab")
+        ntab = const.tile([P, 2, 256], F32, name="ntab")
+        bias_sb = const.tile([P, 2, 16], F32, name="bias_sb")
+        w_rep_q = const.tile([P, 4, P], F32, name="w_rep_q")
+        w_rep_k = const.tile([P, 4, P], F32, name="w_rep_k")
+        ctab_f = ctab[:].rearrange("p r t -> p (r t)")
+        stab_f = stab[:].rearrange("p r t -> p (r t)")
+        ntab_f = ntab[:].rearrange("p r t -> p (r t)")
+
+        def mx(u):
+            n, h = divmod(u, 2)
+            wc, ws = codes_of[n]
+            tok = slice(h * HALF, (h + 1) * HALF)
+            acc = []
+            for e in range(2):
+                pe = ps_mx.tile([P, HALF], F32, name="mx", tag="mx")
+                acc.append(pe)
+                for g in range(PASSES):
+                    c = e * PASSES + g
+                    nc.tensor.matmul_mx(
+                        out=pe[:],
+                        lhsT=wc[:, c * P : (c + 1) * P].bitcast(FP8X4),
+                        lhsT_scale=ws[:, c * P : (c + 1) * P],
+                        rhs=xc[:, g, tok].bitcast(FP8X4),
+                        rhs_scale=xs[:, g, tok],
+                        start=(g == 0),
+                        stop=(g == PASSES - 1),
+                    )
+            acc_of[u] = acc
+
+        def rp_shared(u):
+            j = order[u // 2]
+            acc = acc_of[u]
+            prods = []
+            for i in range(4):
+                t = tpool.tile([P, HALF], F32, name="t%d" % i, tag="t%d" % i)
+                prods.append(t)
+            odd = tpool.tile([P, HALF], F32, name="odd", tag="odd")
+            nc.scalar.activation(out=odd[:], in_=acc[1][:], func=ACT.Identity, bias=bias_sb[:, 1, j : j + 1], scale=1.0)
+            for i, tab in ((0, ctab_f), (2, stab_f)):
+                nc.vector.scalar_tensor_tensor(
+                    out=prods[i][:], in0=acc[0][:], scalar=bias_sb[:, 0, j : j + 1], in1=tab, op0=ALU.add, op1=ALU.mult
+                )
+            for i, tab in ((1, ntab_f), (3, ctab_f)):
+                nc.gpsimd.tensor_tensor(out=prods[i][:], in0=odd[:], in1=tab, op=ALU.mult)
+            prods_of[u] = prods
+
+        def rp(u, pieces=1):
+            j = order[u // 2]
+            acc = acc_of[u]
+            prods = []
+            for i in range(4):
+                t = tpool.tile([P, HALF], F32, name="t%d" % i, tag="t%d" % i)
+                prods.append(t)
+            width = HALF // pieces
+            for c in range(pieces):
+                cols = slice(c * width, (c + 1) * width)
+                for i, (e, tab) in enumerate(((0, ctab_f), (1, ntab_f), (0, stab_f), (1, ctab_f))):
+                    nc.vector.scalar_tensor_tensor(
+                        out=prods[i][:, cols], in0=acc[e][:, cols], scalar=bias_sb[:, e, j : j + 1], in1=tab[:, cols],
+                        op0=ALU.add, op1=ALU.mult,
+                    )
+            prods_of[u] = prods
+
+        def ot(u, b2, where="ot"):
+            prods = prods_of[u]
+            bank = head_bank(where)
+            ots_of.setdefault(u, []).append(bank)
+            for bb in range(2):
+                cols = slice((2 * b2 + bb) * P, (2 * b2 + bb + 1) * P)
+                for half in range(2):
+                    nc.tensor.matmul(
+                        out=bank[:, bb, half, :], lhsT=prods[2 * half][:, cols], rhs=ident[:],
+                        start=True, stop=False, is_transpose=True,
+                    )
+                    nc.tensor.matmul(
+                        out=bank[:, bb, half, :], lhsT=prods[2 * half + 1][:, cols], rhs=ident[:],
+                        start=False, stop=True, is_transpose=True,
+                    )
+
+        def sq(u, b2):
+            if b2 == 0:
+                ss = spool.tile([P, 16], F32, name="ss", tag="ss")
+                ss_of[u] = ss
+                rstd = spool.tile([P, 16], F32, name="rstd", tag="rstd")
+                rstd_of[u] = rstd
+            for bb in range(2):
+                for hh in range(2):
+                    col = 8 * b2 + 2 * bb + hh
+                    junk = spool.tile([P, 2, 64], F32, name="junk", tag="junk")
+                    nc.scalar.activation(
+                        out=junk[:], in_=ots_of[u][b2][:, bb, :, hh * 64 : (hh + 1) * 64], func=ACT.Square,
+                        accum_out=ss_of[u][:, col : col + 1],
+                    )
+
+        def rs(u, b2):
+            nc.scalar.activation(
+                out=rstd_of[u][:, 8 * b2 : 8 * b2 + 4], in_=ss_of[u][:, 8 * b2 : 8 * b2 + 4],
+                func=ACT.Abs_reciprocal_sqrt, bias=EPS, scale=1.0 / 128.0,
+            )
+
+        def rs_unit(u):
+            nc.scalar.activation(
+                out=rstd_of[u][:].rearrange("p (b c) -> p b c", b=2)[:, :, 0:4],
+                in_=ss_of[u][:].rearrange("p (b c) -> p b c", b=2)[:, :, 0:4],
+                func=ACT.Abs_reciprocal_sqrt, bias=EPS, scale=1.0 / 128.0,
+            )
+
+        def ot_sq(u):
+            ot(u, 0)
+            ot(u, 1)
+            sq(u, 0)
+            sq(u, 1)
+            rs_unit(u)
+
+        def finish(u, b2, on_vector):
+            n, h = divmod(u, 2)
+            j = order[n]
+            bank = ots_of[u][b2]
+            rstd = rstd_of[u]
+            wr = w_rep_q if j < N_Q_PAIRS else w_rep_k
+            if j < N_Q_PAIRS:
+                dst = oq_view[:, 4 * h : 4 * h + 4, 256 * j : 256 * (j + 1)]
+            else:
+                dst = ok_view[:, 4 * h : 4 * h + 4, 256 * (j - N_Q_PAIRS) : 256 * (j - N_Q_PAIRS + 1)]
+            if b2 == 0:
+                y = ypool.tile([P, 4, 2, P], F32, name="y", tag="y")
+                y_of[u] = y
+            y = y_of[u]
+            yf = y[:].rearrange("p b h d -> p (b h d)")
+            for bb in range(2):
+                for hh in range(2):
+                    blk = 2 * b2 + bb
+                    col = 8 * b2 + 2 * bb + hh
+                    if on_vector:
+                        nc.vector.scalar_tensor_tensor(
+                            out=y[:, blk, hh, :].rearrange("p (a i) -> p a i", a=2),
+                            in0=bank[:, bb, :, hh * 64 : (hh + 1) * 64],
+                            scalar=rstd[:, col : col + 1],
+                            in1=wr[:, 0, :].rearrange("p (a i) -> p a i", a=2),
+                            op0=ALU.mult,
+                            op1=ALU.mult,
+                        )
+                    else:
+                        nc.scalar.activation(
+                            out=y[:, blk, hh, :].rearrange("p (a i) -> p a i", a=2),
+                            in_=bank[:, bb, :, hh * 64 : (hh + 1) * 64],
+                            func=ACT.Copy,
+                            scale=rstd[:, col : col + 1],
+                        )
+            if not on_vector:
+                nc.gpsimd.tensor_tensor(
+                    out=yf[:, b2 * 512 : (b2 + 1) * 512],
+                    in0=yf[:, b2 * 512 : (b2 + 1) * 512],
+                    in1=wr[:].rearrange("p r d -> p (r d)"),
+                    op=ALU.mult,
+                )
+            nc.sync.dma_start(
+                out=dst[:, 2 * b2 : 2 * b2 + 2, :],
+                in_=y[:, 2 * b2 : 2 * b2 + 2, :, :].rearrange("p b h d -> p b (h d)"),
+            )
+
+        load_w(0)
+        for c in range(2):
+            nc.sync.dma_start(
+                out=sc_bc[:, c * 1024 : (c + 1) * 1024],
+                in_=Wq_scale.rearrange("o k -> (o k)")[c * 1024 : (c + 1) * 1024].partition_broadcast(P),
+            )
+        nc.sync.dma_start(out=brow_bf[0:N_Q_PAIRS, :], in_=bq.rearrange("(j c) -> j c", c=256))
+        nc.sync.dma_start(
+            out=brow_bf[N_Q_PAIRS : N_Q_PAIRS + N_K_PAIRS, :], in_=bk.rearrange("(j c) -> j c", c=256)
+        )
+        for kind, i in (("x", 0), ("x", 1), ("x", 2), ("x", 3), ("w", 1), ("x", 4), ("x", 5), ("x", 6), ("x", 7), ("w", 2), ("w", 3), ("w", 4)):
+            if kind == "x":
+                load_x(i)
+            else:
+                load_w(i)
+        nc.sync.dma_start(out=wq_bc[:], in_=qn_w.partition_broadcast(P))
+        nc.sync.dma_start(out=wk_bc[:], in_=kn_w.partition_broadcast(P))
+        state = {"p": 0, "l": 5}
+        qhalves = [2 * n + e for n in range(N_PAIRS) for e in range(2) if order[n] < N_Q_PAIRS]
+
+        def more_loads():
+            if state["l"] < N_PAIRS:
+                load_w(state["l"])
+                state["l"] += 1
+
+        def next_prod(c=1):
+            for i in range(c):
+                if state["p"] < len(qhalves):
+                    n, e = divmod(qhalves[state["p"]], 2)
+                    prod(n, e)
+                    state["p"] += 1
+                    if e == 1:
+                        more_loads()
+
+        def due(k):
+            return state["p"] < len(qhalves) and qhalves[state["p"]] <= k + 5
+
+        setup_widen()
+        setup_tables()
+        setup_bias()
+        for c in range(2):
+            for e in range(2):
+                prod(0, e, c * 1024, (c + 1) * 1024)
+        state["p"] = 2
+        more_loads()
+        xt_(0, ("mx", "mx"))
+        xt_(1, ("mx", "mx"))
+        qx(0, 0)
+        bt(0, False, ("mx", "mx"))
+        xt_(2, ("mx", "mx"))
+        bt(1, False, ("mx", "mx"))
+        xt_(3, ("mx", "mx"))
+        next_prod(1)
+        qw(0)
+        qx(0, 1)
+        xt_(4, ("tp", "ot"))
+        xt_(5, ("tp", "ot"))
+        mx(0)
+        next_prod(1)
+        bt(2, False, ("tp", "ot"))
+        qx(1, 0)
+        xt_(6, ("tp", "ot"))
+        xt_(7, ("tp", "ot"))
+        bt(3, False, ("tp", "ot"))
+        rp(0)
+        qx(1, 1)
+        mx(1)
+        setup_gains()
+        qw(1)
+        next_prod(1)
+        rp(1)
+        ot_sq(0)
+        bt(4, False)
+
+        for k in range(1, N_UNITS):
+            by_vector = k - 1 >= N_UNITS - V_TAIL
+            if k + 1 < N_UNITS:
+                mx(k + 1)
+            if due(k) or k % 2 == 1:
+                next_prod()
+            if not by_vector:
+                finish(k - 1, 0, False)
+                finish(k - 1, 1, False)
+            m = k + 4
+            if m < 2 * N_PAIRS:
+                if order[m // 2] >= N_Q_PAIRS and m % 2 == 1:
+                    more_loads()
+                bt(m, False)
+            if k + 1 < N_UNITS:
+                if False:
+                    rp_shared(k + 1)
+                else:
+                    rp(k + 1, 2 if k + 1 == N_UNITS - 1 else 1)
+            if by_vector:
+                finish(k - 1, 0, True)
+                finish(k - 1, 1, True)
+            where = "tp" if (k >= N_UNITS - 4 and k % 2 == 1) else "ot"
+            if k < N_UNITS - 1:
+                ot(k, 0, where)
+                ot(k, 1, where)
+                sq(k, 0)
+                sq(k, 1)
+                rs_unit(k)
+            else:
+                for b2 in range(2):
+                    ot(k, b2, where)
+                    sq(k, b2)
+                    rs(k, b2)
+                    finish(k, b2, True)
+            flush_late()
+            if (k + 3) % 2 == 0 and (k + 3) // 2 < N_PAIRS:
+                qw((k + 3) // 2)

@@ -37,6 +37,7 @@ def tile_gqaselfattention_pa_kernel(
     oq_view = out_0.rearrange("b t h d -> (b t) (h d)").rearrange("(n p) c -> p n c", p=P)
     ok_view = out_1.rearrange("b t h d -> (b t) (h d)").rearrange("(n p) c -> p n c", p=P)
     order = [0, 1, 8, 2, 3, 4, 9, 5, 6, 7]
+    units = [(n, h) for n in range(N_PAIRS) for h in range(2)]
 
     with ExitStack() as ctx:
         const = ctx.enter_context(tc.tile_pool(name="const", bufs=1))
@@ -53,16 +54,19 @@ def tile_gqaselfattention_pa_kernel(
         ps_mx = ctx.enter_context(tc.psum_pool(name="ps_mx", bufs=4))
         ps_ot = ctx.enter_context(tc.psum_pool(name="ps_ot", bufs=2))
 
-        cs_bf = const.tile([P, 2, 2, 64], BF16, name="cs_bf")
+        cs_bf = const.tile([P, 2, 2, 2, 64], BF16, name="cs_bf")
         brow_bf = const.tile([P, 256], BF16, name="brow_bf")
         warm = const.tile([P, 1], F32, name="warm")
         warm_out = const.tile([P, 1], F32, name="warm_out")
         ident = const.tile([P, P], F32, name="ident")
+        ident_bf = const.tile([P, P], BF16, name="ident_bf")
         sc_bc = const.tile([P, K], F32, name="sc_bc")
+        sc_k = const.tile([P, PASSES, 4], F32, name="sc_k")
         wq_bc = const.tile([P, P], BF16, name="wq_bc")
         wk_bc = const.tile([P, P], BF16, name="wk_bc")
         nc.vector.memset(brow_bf[:], 0.0)
         nc.vector.memset(warm[:], 1.0)
+        make_identity(nc, ident_bf[:])
         make_identity(nc, ident[:])
 
         x_sb = []
@@ -78,8 +82,9 @@ def tile_gqaselfattention_pa_kernel(
 
         ctx.enter_context(tc.manual_schedule())
 
-        nc.sync.dma_start(out=cs_bf[:, 0, :, :], in_=cos.rearrange("(b p) i -> p b i", p=P))
-        nc.sync.dma_start(out=cs_bf[:, 1, :, :], in_=sin.rearrange("(b p) i -> p b i", p=P))
+        for c, src in ((0, cos), (1, sin)):
+            for hh in range(2):
+                nc.sync.dma_start(out=cs_bf[:, c, :, hh, :], in_=src.rearrange("(b p) i -> p b i", p=P))
         nc.scalar.activation(out=warm_out[:], in_=warm[:], func=ACT.Abs_reciprocal_sqrt)
 
         wb_of = {}
@@ -92,7 +97,6 @@ def tile_gqaselfattention_pa_kernel(
         ss_of = {}
         rstd_of = {}
         y_of = {}
-        late = []
 
         def load_x(i):
             nc.sync.dma_start(out=x_sb[i][:], in_=x_view[i])
@@ -108,6 +112,18 @@ def tile_gqaselfattention_pa_kernel(
                 by_of[n] = by
                 nc.sync.dma_start(out=by[:], in_=wq_view[j])
 
+        plain = set()
+
+        def widen(n, e, engine):
+            if n not in wb_of:
+                wb = wbpool.tile([P, 2, K], BF16, name="wb", tag="wb")
+                wb_of[n] = wb
+            plain.add(2 * n + e)
+            if engine is nc.scalar:
+                nc.scalar.copy(out=wb_of[n][:, e, :], in_=by_of[n][:, e, :].bitcast(FP8))
+            else:
+                engine.tensor_copy(out=wb_of[n][:, e, :], in_=by_of[n][:, e, :].bitcast(FP8))
+
         def prod(n, e, lo=0, hi=K):
             if n not in wb_of:
                 wb = wbpool.tile([P, 2, K], BF16, name="wb", tag="wb")
@@ -115,11 +131,6 @@ def tile_gqaselfattention_pa_kernel(
             nc.vector.tensor_tensor(
                 out=wb_of[n][:, e, lo:hi], in0=by_of[n][:, e, lo:hi].bitcast(FP8), in1=sc_bc[:, lo:hi], op=ALU.mult
             )
-
-        def flush_late():
-            for tp, dst in late:
-                nc.scalar.copy(out=dst, in_=tp[:].rearrange("p g u r -> p g r u"))
-            late.clear()
 
         def head_bank(where):
             if where == "mx":
@@ -130,7 +141,18 @@ def tile_gqaselfattention_pa_kernel(
                 bank = ps_tp.tile([P, 2, 2, P], F32, name="tp", tag="tp")
             return bank
 
-        def transpose_rows(src_bf, dst_words, defer, where=("tp", "tp")):
+        def scaled_exit(tp, dst, gp):
+            nc.vector.tensor_tensor(
+                out=dst.rearrange("p g r (u e) -> p g r u e", e=2),
+                in0=tp[:].bitcast(BF16).rearrange("p u g (r e) -> p g r u e", e=2),
+                in1=sc_k[:, 2 * gp : 2 * gp + 2, :]
+                .rearrange("p g (u e) -> p g u e", e=2)
+                .unsqueeze(2)
+                .to_broadcast([P, 2, P, 2, 2]),
+                op=ALU.mult,
+            )
+
+        def transpose_rows(src_bf, dst, vx, where=("tp", "tp")):
             words = src_bf.bitcast(F32)
             for gp in range(2):
                 tp = head_bank(where[gp])
@@ -138,15 +160,19 @@ def tile_gqaselfattention_pa_kernel(
                     g = 2 * gp + g2
                     for u in range(2):
                         nc.tensor.transpose(
-                            tp[:, g2, u, :], words[:, 256 * g + u : 256 * (g + 1) : 2], ident[:]
+                            tp[:, u, g2, :], words[:, 256 * g + u : 256 * (g + 1) : 2], ident[:]
                         )
-                late.append((tp, dst_words[:, 2 * gp : 2 * gp + 2, :, :]))
-                if not (defer and gp == 1):
-                    flush_late()
+                if vx == "scaled":
+                    scaled_exit(tp, dst[:, 2 * gp : 2 * gp + 2, :, :], gp)
+                    continue
+                (nc.vector.tensor_copy if gp in vx else nc.scalar.copy)(
+                    out=dst.bitcast(F32)[:, 2 * gp : 2 * gp + 2, :, :],
+                    in_=tp[:].rearrange("p u g r -> p g r u"),
+                )
 
         def xt_(i, where):
             h, tl = divmod(i, 4)
-            transpose_rows(x_sb[i][:], xg[h][:].bitcast(F32)[:, :, tl * P : (tl + 1) * P, :], False, where)
+            transpose_rows(x_sb[i][:], xg[h][:, :, tl * P : (tl + 1) * P, :], (lambda i: ())(i), where)
 
         def qx(h, tp2):
             for g in range(PASSES):
@@ -157,12 +183,12 @@ def tile_gqaselfattention_pa_kernel(
                     in_=xg[h][:, g, tp2 * 256 : (tp2 + 1) * 256, :].rearrange("p n t -> p (n t)"),
                 )
 
-        def bt(m, defer, where=("tp", "tp")):
+        def bt(m, where=("tp", "tp")):
             n, e = divmod(m, 2)
             if e == 0:
                 wg = gpool.tile([P, 2, PASSES, P, 4], BF16, name="wg", tag="wg", align_bytes=64)
                 wg_of[n] = wg
-            transpose_rows(wb_of[n][:, e, :], wg_of[n][:].bitcast(F32)[:, e, :, :, :], defer, where)
+            transpose_rows(wb_of[n][:, e, :], wg_of[n][:, e, :, :, :], "scaled" if m in plain else (lambda m: ())(m), where)
 
         def qw(n):
             wc = wpool.tile([P, 2 * PASSES * P], U32, name="wc", tag="wc", align_bytes=64)
@@ -172,50 +198,39 @@ def tile_gqaselfattention_pa_kernel(
             )
             codes_of[n] = (wc, ws)
 
-        cs_f = const.tile([P, 2, 2, 2, 64], F32, name="cs_f")
-        brow_f = const.tile([P, 256], F32, name="brow_f")
-
-        def setup_widen():
-            for hh in range(2):
-                nc.scalar.copy(out=cs_f[:, :, :, hh, :], in_=cs_bf[:])
+        tabs = const.tile([P, 2, 256], F32, name="tabs")
+        ntab = const.tile([P, 256], F32, name="ntab")
 
         def setup_tables():
-            tp_cs = ps_ot.tile([P, 2, 2, P], F32, name="ot", tag="ot")
+            tp_cs = ps_ot.tile([P, 2, 2, P], BF16, name="ot", tag="ot")
             for c in range(2):
                 for b in range(2):
                     nc.tensor.transpose(
-                        tp_cs[:, c, b, :], cs_f[:, c, b, :, :].rearrange("p h i -> p (h i)"), ident[:]
+                        tp_cs[:, c, b, :], cs_bf[:, c, b, :, :].rearrange("p h i -> p (h i)"), ident_bf[:]
                     )
-            for rep in range(2):
-                nc.scalar.copy(out=ctab[:, rep, :], in_=tp_cs[:, 0, :, :].rearrange("p b t -> p (b t)"))
-                nc.scalar.copy(out=stab[:, rep, :], in_=tp_cs[:, 1, :, :].rearrange("p b t -> p (b t)"))
-                nc.scalar.mul(out=ntab[:, rep, :], in_=tp_cs[:, 1, :, :].rearrange("p b t -> p (b t)"), mul=-1.0)
+            nc.vector.tensor_copy(out=tabs[:], in_=tp_cs[:].rearrange("p c b t -> p c (b t)"))
+            nc.vector.tensor_scalar(
+                out=ntab[:], in0=tp_cs[:, 1, :, :].rearrange("p b t -> p (b t)"), scalar1=-1.0, scalar2=None, op0=ALU.mult
+            )
+
+        def table(i, reps):
+            tab = (tabs[:, 0, :], ntab[:], tabs[:, 1, :], tabs[:, 0, :])[i]
+            return tab.unsqueeze(1).to_broadcast([P, reps, 256])
+
+        bias_sb = const.tile([P, 2, N_PAIRS], F32, name="bias_sb")
 
         def setup_bias():
-            nc.scalar.copy(out=brow_f[:], in_=brow_bf[:])
-            tp_b = ps_ot.tile([P, 2, 2, P], F32, name="ot", tag="ot")
-            brow_v = brow_f[:].rearrange("p (c e) -> p e c", e=2)
+            tp_b = ps_ot.tile([P, 2, P], BF16, name="ot", tag="ot")
+            brow_v = brow_bf[:].rearrange("p (c e) -> p e c", e=2)
             for e in range(2):
-                nc.tensor.transpose(tp_b[:, 0, e, :], brow_v[:, e, :], ident[:])
-            nc.scalar.copy(out=bias_sb[:, :, 0:10], in_=tp_b[:, 0, :, 0:10])
+                nc.tensor.transpose(tp_b[:, e, :], brow_v[:, e, :], ident_bf[:])
+            nc.vector.tensor_copy(out=bias_sb[:], in_=tp_b[:, :, 0:N_PAIRS])
 
-        def setup_gains():
-            for wr, src in ((w_rep_q, wq_bc), (w_rep_k, wk_bc)):
-                for r in range(4):
-                    nc.gpsimd.tensor_copy(out=wr[:, r, :], in_=src[:])
-
-        ctab = const.tile([P, 2, 256], F32, name="ctab")
-        stab = const.tile([P, 2, 256], F32, name="stab")
-        ntab = const.tile([P, 2, 256], F32, name="ntab")
-        bias_sb = const.tile([P, 2, 16], F32, name="bias_sb")
-        w_rep_q = const.tile([P, 4, P], F32, name="w_rep_q")
-        w_rep_k = const.tile([P, 4, P], F32, name="w_rep_k")
-        ctab_f = ctab[:].rearrange("p r t -> p (r t)")
-        stab_f = stab[:].rearrange("p r t -> p (r t)")
-        ntab_f = ntab[:].rearrange("p r t -> p (r t)")
+        def bias_of(j, e):
+            return bias_sb[:, e, j : j + 1]
 
         def mx(u):
-            n, h = divmod(u, 2)
+            n, h = units[u]
             wc, ws = codes_of[n]
             tok = slice(h * HALF, (h + 1) * HALF)
             acc = []
@@ -235,37 +250,21 @@ def tile_gqaselfattention_pa_kernel(
                     )
             acc_of[u] = acc
 
-        def rp_shared(u):
-            j = order[u // 2]
-            acc = acc_of[u]
-            prods = []
-            for i in range(4):
-                t = tpool.tile([P, HALF], F32, name="t%d" % i, tag="t%d" % i)
-                prods.append(t)
-            odd = tpool.tile([P, HALF], F32, name="odd", tag="odd")
-            nc.scalar.activation(out=odd[:], in_=acc[1][:], func=ACT.Identity, bias=bias_sb[:, 1, j : j + 1], scale=1.0)
-            for i, tab in ((0, ctab_f), (2, stab_f)):
-                nc.vector.scalar_tensor_tensor(
-                    out=prods[i][:], in0=acc[0][:], scalar=bias_sb[:, 0, j : j + 1], in1=tab, op0=ALU.add, op1=ALU.mult
-                )
-            for i, tab in ((1, ntab_f), (3, ctab_f)):
-                nc.gpsimd.tensor_tensor(out=prods[i][:], in0=odd[:], in1=tab, op=ALU.mult)
-            prods_of[u] = prods
-
         def rp(u, pieces=1):
-            j = order[u // 2]
+            j = order[units[u][0]]
             acc = acc_of[u]
             prods = []
             for i in range(4):
                 t = tpool.tile([P, HALF], F32, name="t%d" % i, tag="t%d" % i)
                 prods.append(t)
-            width = HALF // pieces
+            reps = 2 // pieces
             for c in range(pieces):
-                cols = slice(c * width, (c + 1) * width)
-                for i, (e, tab) in enumerate(((0, ctab_f), (1, ntab_f), (0, stab_f), (1, ctab_f))):
+                cols = slice(c * 256 * reps, (c + 1) * 256 * reps)
+                for i, e in ((0, 0), (2, 0), (1, 1), (3, 1)):
                     nc.vector.scalar_tensor_tensor(
-                        out=prods[i][:, cols], in0=acc[e][:, cols], scalar=bias_sb[:, e, j : j + 1], in1=tab[:, cols],
-                        op0=ALU.add, op1=ALU.mult,
+                        out=prods[i][:, cols].rearrange("p (r t) -> p r t", t=256),
+                        in0=acc[e][:, cols].rearrange("p (r t) -> p r t", t=256),
+                        scalar=bias_of(j, e), in1=table(i, reps), op0=ALU.add, op1=ALU.mult,
                     )
             prods_of[u] = prods
 
@@ -285,14 +284,14 @@ def tile_gqaselfattention_pa_kernel(
                         start=False, stop=True, is_transpose=True,
                     )
 
-        def sq(u, b2):
-            if b2 == 0:
+        def sq(u, b2, pieces=(0, 1, 2, 3)):
+            if b2 == 0 and pieces[0] == 0:
                 ss = spool.tile([P, 16], F32, name="ss", tag="ss")
                 ss_of[u] = ss
                 rstd = spool.tile([P, 16], F32, name="rstd", tag="rstd")
                 rstd_of[u] = rstd
-            for bb in range(2):
-                for hh in range(2):
+            for i in pieces:
+                    bb, hh = divmod(i, 2)
                     col = 8 * b2 + 2 * bb + hh
                     junk = spool.tile([P, 2, 64], F32, name="junk", tag="junk")
                     nc.scalar.activation(
@@ -320,23 +319,22 @@ def tile_gqaselfattention_pa_kernel(
             sq(u, 1)
             rs_unit(u)
 
-        def finish(u, b2, on_vector):
-            n, h = divmod(u, 2)
+        def finish(u, b2, on_vector, pieces=(0, 1, 2, 3)):
+            n, h = units[u]
             j = order[n]
             bank = ots_of[u][b2]
             rstd = rstd_of[u]
-            wr = w_rep_q if j < N_Q_PAIRS else w_rep_k
+            gain = wq_bc if j < N_Q_PAIRS else wk_bc
             if j < N_Q_PAIRS:
                 dst = oq_view[:, 4 * h : 4 * h + 4, 256 * j : 256 * (j + 1)]
             else:
                 dst = ok_view[:, 4 * h : 4 * h + 4, 256 * (j - N_Q_PAIRS) : 256 * (j - N_Q_PAIRS + 1)]
-            if b2 == 0:
+            if b2 == 0 and pieces[0] == 0:
                 y = ypool.tile([P, 4, 2, P], F32, name="y", tag="y")
                 y_of[u] = y
             y = y_of[u]
-            yf = y[:].rearrange("p b h d -> p (b h d)")
-            for bb in range(2):
-                for hh in range(2):
+            for i in pieces:
+                    bb, hh = divmod(i, 2)
                     blk = 2 * b2 + bb
                     col = 8 * b2 + 2 * bb + hh
                     if on_vector:
@@ -344,7 +342,7 @@ def tile_gqaselfattention_pa_kernel(
                             out=y[:, blk, hh, :].rearrange("p (a i) -> p a i", a=2),
                             in0=bank[:, bb, :, hh * 64 : (hh + 1) * 64],
                             scalar=rstd[:, col : col + 1],
-                            in1=wr[:, 0, :].rearrange("p (a i) -> p a i", a=2),
+                            in1=gain[:].rearrange("p (a i) -> p a i", a=2),
                             op0=ALU.mult,
                             op1=ALU.mult,
                         )
@@ -355,35 +353,36 @@ def tile_gqaselfattention_pa_kernel(
                             func=ACT.Copy,
                             scale=rstd[:, col : col + 1],
                         )
+            if pieces[-1] != 3:
+                return
             if not on_vector:
+                yb = y[:, 2 * b2 : 2 * b2 + 2, :, :].rearrange("p b h d -> p (b h) d")
                 nc.gpsimd.tensor_tensor(
-                    out=yf[:, b2 * 512 : (b2 + 1) * 512],
-                    in0=yf[:, b2 * 512 : (b2 + 1) * 512],
-                    in1=wr[:].rearrange("p r d -> p (r d)"),
-                    op=ALU.mult,
+                    out=yb, in0=yb, in1=gain[:].unsqueeze(1).to_broadcast([P, 4, P]), op=ALU.mult
                 )
             nc.sync.dma_start(
                 out=dst[:, 2 * b2 : 2 * b2 + 2, :],
                 in_=y[:, 2 * b2 : 2 * b2 + 2, :, :].rearrange("p b h d -> p b (h d)"),
             )
 
-        load_w(0)
-        for c in range(2):
-            nc.sync.dma_start(
-                out=sc_bc[:, c * 1024 : (c + 1) * 1024],
-                in_=Wq_scale.rearrange("o k -> (o k)")[c * 1024 : (c + 1) * 1024].partition_broadcast(P),
-            )
-        nc.sync.dma_start(out=brow_bf[0:N_Q_PAIRS, :], in_=bq.rearrange("(j c) -> j c", c=256))
-        nc.sync.dma_start(
-            out=brow_bf[N_Q_PAIRS : N_Q_PAIRS + N_K_PAIRS, :], in_=bk.rearrange("(j c) -> j c", c=256)
-        )
-        for kind, i in (("x", 0), ("x", 1), ("x", 2), ("x", 3), ("w", 1), ("x", 4), ("x", 5), ("x", 6), ("x", 7), ("w", 2), ("w", 3), ("w", 4)):
+        for kind, i in (("w", 0), ("s", 0), ("s", 1), ("b", 0), ("x", 0), ("x", 1), ("x", 2), ("x", 3), ("w", 1), ("x", 4), ("x", 5), ("x", 6), ("x", 7), ("w", 2), ("w", 3), ("w", 4), ("g", 0)):
             if kind == "x":
                 load_x(i)
-            else:
+            elif kind == "w":
                 load_w(i)
-        nc.sync.dma_start(out=wq_bc[:], in_=qn_w.partition_broadcast(P))
-        nc.sync.dma_start(out=wk_bc[:], in_=kn_w.partition_broadcast(P))
+            elif kind == "s":
+                nc.sync.dma_start(
+                    out=sc_bc[:, i * 1024 : (i + 1) * 1024],
+                    in_=Wq_scale.rearrange("o k -> (o k)")[i * 1024 : (i + 1) * 1024].partition_broadcast(P),
+                )
+            elif kind == "k":
+                nc.sync.dma_start(out=sc_k[:], in_=Wq_scale.rearrange("o (g p t) -> p (o g) t", p=P, t=4))
+            elif kind == "b":
+                nc.sync.dma_start(out=brow_bf[0:N_Q_PAIRS, :], in_=bq.rearrange("(j c) -> j c", c=256))
+                nc.sync.dma_start(out=brow_bf[N_Q_PAIRS:N_PAIRS, :], in_=bk.rearrange("(j c) -> j c", c=256))
+            else:
+                nc.sync.dma_start(out=wq_bc[:], in_=qn_w.partition_broadcast(P))
+                nc.sync.dma_start(out=wk_bc[:], in_=kn_w.partition_broadcast(P))
         state = {"p": 0, "l": 5}
         qhalves = [2 * n + e for n in range(N_PAIRS) for e in range(2) if order[n] < N_Q_PAIRS]
 
@@ -404,9 +403,15 @@ def tile_gqaselfattention_pa_kernel(
         def due(k):
             return state["p"] < len(qhalves) and qhalves[state["p"]] <= k + 5
 
-        setup_widen()
+        def next_widen(engine):
+            n, e = divmod(qhalves[state["p"]], 2)
+            widen(n, e, engine)
+            state["p"] += 1
+            if e == 1:
+                more_loads()
+
+        shared = lambda u: False
         setup_tables()
-        setup_bias()
         for c in range(2):
             for e in range(2):
                 prod(0, e, c * 1024, (c + 1) * 1024)
@@ -415,51 +420,53 @@ def tile_gqaselfattention_pa_kernel(
         xt_(0, ("mx", "mx"))
         xt_(1, ("mx", "mx"))
         qx(0, 0)
-        bt(0, False, ("mx", "mx"))
+        bt(0, ("mx", "mx"))
         xt_(2, ("mx", "mx"))
-        bt(1, False, ("mx", "mx"))
+        bt(1, ("mx", "mx"))
         xt_(3, ("mx", "mx"))
         next_prod(1)
         qw(0)
         qx(0, 1)
         xt_(4, ("tp", "ot"))
         xt_(5, ("tp", "ot"))
+        setup_bias()
         mx(0)
         next_prod(1)
-        bt(2, False, ("tp", "ot"))
+        bt(2, ("tp", "ot"))
         qx(1, 0)
         xt_(6, ("tp", "ot"))
         xt_(7, ("tp", "ot"))
-        bt(3, False, ("tp", "ot"))
+        bt(3, ("tp", "ot"))
         rp(0)
         qx(1, 1)
         mx(1)
-        setup_gains()
         qw(1)
         next_prod(1)
         rp(1)
-        ot_sq(0)
-        bt(4, False)
-
+        ot(0, 0)
+        ot(0, 1)
+        sq(0, 0)
+        rs(0, 0)
+        sq(0, 1)
+        bt(4, ("tp", "tp"))
         for k in range(1, N_UNITS):
-            by_vector = k - 1 >= N_UNITS - V_TAIL
+            by_vector = k - 1 >= N_UNITS - 2
             if k + 1 < N_UNITS:
                 mx(k + 1)
             if due(k) or k % 2 == 1:
                 next_prod()
             if not by_vector:
-                finish(k - 1, 0, False)
+                finish(k - 1, 0, False, (0, 1))
+                rs(k - 1, 1)
+                finish(k - 1, 0, False, (2, 3))
                 finish(k - 1, 1, False)
             m = k + 4
             if m < 2 * N_PAIRS:
                 if order[m // 2] >= N_Q_PAIRS and m % 2 == 1:
                     more_loads()
-                bt(m, False)
+                bt(m)
             if k + 1 < N_UNITS:
-                if False:
-                    rp_shared(k + 1)
-                else:
-                    rp(k + 1, 2 if k + 1 == N_UNITS - 1 else 1)
+                rp(k + 1, 2 if k + 1 == N_UNITS - 1 else 1)
             if by_vector:
                 finish(k - 1, 0, True)
                 finish(k - 1, 1, True)
@@ -468,14 +475,18 @@ def tile_gqaselfattention_pa_kernel(
                 ot(k, 0, where)
                 ot(k, 1, where)
                 sq(k, 0)
-                sq(k, 1)
-                rs_unit(k)
+                if k < N_UNITS - 2:
+                    sq(k, 1, (0, 1))
+                    rs(k, 0)
+                    sq(k, 1, (2, 3))
+                else:
+                    sq(k, 1)
+                    rs_unit(k)
             else:
                 for b2 in range(2):
                     ot(k, b2, where)
                     sq(k, b2)
                     rs(k, b2)
                     finish(k, b2, True)
-            flush_late()
             if (k + 3) % 2 == 0 and (k + 3) // 2 < N_PAIRS:
                 qw((k + 3) // 2)

@@ -73,8 +73,8 @@ def tile_gqaselfattention_pa_kernel(
         for n in range(8):
             xt = xin.tile([P, K], BF16, name="x_sb", tag="x_sb")
             x_sb.append(xt)
-        xc = xkeep.tile([P, PASSES, TOKENS], U32, name="xc", align_bytes=64)
-        xs = xkeep.tile([P, PASSES, TOKENS], U8, name="xs", align_bytes=64)
+        xc = xkeep.tile([P, 2, PASSES, HALF], U32, name="xc", align_bytes=64)
+        xs = xkeep.tile([P, 2, PASSES, HALF], U8, name="xs", align_bytes=64)
         xg = []
         for h in range(2):
             xgh = xkeep.tile([P, PASSES, HALF, 4], BF16, name="xg%d" % h, align_bytes=64)
@@ -152,6 +152,13 @@ def tile_gqaselfattention_pa_kernel(
                 op=ALU.mult,
             )
 
+        held = []
+
+        def flush(c=2):
+            for i in range(min(c, len(held))):
+                tp, dst = held.pop(0)
+                nc.scalar.copy(out=dst, in_=tp[:].rearrange("p u g r -> p g r u"))
+
         def transpose_rows(src_bf, dst, vx, where=("tp", "tp")):
             words = src_bf.bitcast(F32)
             for gp in range(2):
@@ -165,6 +172,9 @@ def tile_gqaselfattention_pa_kernel(
                 if vx == "scaled":
                     scaled_exit(tp, dst[:, 2 * gp : 2 * gp + 2, :, :], gp)
                     continue
+                if vx == "hold":
+                    held.append((tp, dst.bitcast(F32)[:, 2 * gp : 2 * gp + 2, :, :]))
+                    continue
                 (nc.vector.tensor_copy if gp in vx else nc.scalar.copy)(
                     out=dst.bitcast(F32)[:, 2 * gp : 2 * gp + 2, :, :],
                     in_=tp[:].rearrange("p u g r -> p g r u"),
@@ -175,20 +185,27 @@ def tile_gqaselfattention_pa_kernel(
             transpose_rows(x_sb[i][:], xg[h][:, :, tl * P : (tl + 1) * P, :], (lambda i: ())(i), where)
 
         def qx(h, tp2):
+            cols = slice(tp2 * 256, (tp2 + 1) * 256)
             for g in range(PASSES):
-                lo = h * HALF + tp2 * 256
                 nc.vector.quantize_mx(
-                    out=xc[:, g, lo : lo + 256].bitcast(FP8X4),
-                    scales=xs[:, g, lo : lo + 256],
-                    in_=xg[h][:, g, tp2 * 256 : (tp2 + 1) * 256, :].rearrange("p n t -> p (n t)"),
+                    out=xc[:, h, g, cols].bitcast(FP8X4),
+                    scales=xs[:, h, g, cols],
+                    in_=xg[h][:, g, cols, :].rearrange("p n t -> p (n t)"),
                 )
 
-        def bt(m, where=("tp", "tp")):
+        def qx_wide(h, gp):
+            nc.vector.quantize_mx(
+                out=xc[:, h, 2 * gp : 2 * gp + 2, :].rearrange("p g n -> p (g n)").bitcast(FP8X4),
+                scales=xs[:, h, 2 * gp : 2 * gp + 2, :].rearrange("p g n -> p (g n)"),
+                in_=xg[h][:, 2 * gp : 2 * gp + 2, :, :].rearrange("p g n t -> p (g n t)"),
+            )
+
+        def bt(m, where=("tp", "tp"), hold=False):
             n, e = divmod(m, 2)
             if e == 0:
                 wg = gpool.tile([P, 2, PASSES, P, 4], BF16, name="wg", tag="wg", align_bytes=64)
                 wg_of[n] = wg
-            transpose_rows(wb_of[n][:, e, :], wg_of[n][:, e, :, :, :], "scaled" if m in plain else (lambda m: ())(m), where)
+            transpose_rows(wb_of[n][:, e, :], wg_of[n][:, e, :, :, :], "scaled" if m in plain else ("hold" if hold else (lambda m: ())(m)), where)
 
         def qw(n):
             wc = wpool.tile([P, 2 * PASSES * P], U32, name="wc", tag="wc", align_bytes=64)
@@ -198,8 +215,7 @@ def tile_gqaselfattention_pa_kernel(
             )
             codes_of[n] = (wc, ws)
 
-        tabs = const.tile([P, 2, 256], F32, name="tabs")
-        ntab = const.tile([P, 256], F32, name="ntab")
+        tabs = const.tile([P, 4, 2, 256], F32, name="tabs")
 
         def setup_tables():
             tp_cs = ps_ot.tile([P, 2, 2, P], BF16, name="ot", tag="ot")
@@ -208,14 +224,12 @@ def tile_gqaselfattention_pa_kernel(
                     nc.tensor.transpose(
                         tp_cs[:, c, b, :], cs_bf[:, c, b, :, :].rearrange("p h i -> p (h i)"), ident_bf[:]
                     )
-            nc.vector.tensor_copy(out=tabs[:], in_=tp_cs[:].rearrange("p c b t -> p c (b t)"))
-            nc.vector.tensor_scalar(
-                out=ntab[:], in0=tp_cs[:, 1, :, :].rearrange("p b t -> p (b t)"), scalar1=-1.0, scalar2=None, op0=ALU.mult
-            )
-
-        def table(i, reps):
-            tab = (tabs[:, 0, :], ntab[:], tabs[:, 1, :], tabs[:, 0, :])[i]
-            return tab.unsqueeze(1).to_broadcast([P, reps, 256])
+            cs_t = tp_cs[:].rearrange("p c b t -> p c (b t)")
+            for r in range(2):
+                nc.vector.tensor_copy(out=tabs[:, 0:2, r, :], in_=cs_t)
+            for r in range(2):
+                nc.scalar.mul(out=tabs[:, 2, r, :], in_=cs_t[:, 1, :], mul=-1.0)
+            nc.vector.tensor_copy(out=tabs[:, 3, :, :], in_=tabs[:, 0, :, :])
 
         bias_sb = const.tile([P, 2, N_PAIRS], F32, name="bias_sb")
 
@@ -232,7 +246,6 @@ def tile_gqaselfattention_pa_kernel(
         def mx(u):
             n, h = units[u]
             wc, ws = codes_of[n]
-            tok = slice(h * HALF, (h + 1) * HALF)
             acc = []
             for e in range(2):
                 pe = ps_mx.tile([P, HALF], F32, name="mx", tag="mx")
@@ -243,8 +256,8 @@ def tile_gqaselfattention_pa_kernel(
                         out=pe[:],
                         lhsT=wc[:, c * P : (c + 1) * P].bitcast(FP8X4),
                         lhsT_scale=ws[:, c * P : (c + 1) * P],
-                        rhs=xc[:, g, tok].bitcast(FP8X4),
-                        rhs_scale=xs[:, g, tok],
+                        rhs=xc[:, h, g, :].bitcast(FP8X4),
+                        rhs_scale=xs[:, h, g, :],
                         start=(g == 0),
                         stop=(g == PASSES - 1),
                     )
@@ -252,19 +265,21 @@ def tile_gqaselfattention_pa_kernel(
 
         def rp(u, pieces=1):
             j = order[units[u][0]]
-            acc = acc_of[u]
             prods = []
-            for i in range(4):
-                t = tpool.tile([P, HALF], F32, name="t%d" % i, tag="t%d" % i)
+            for e in range(2):
+                t = tpool.tile([P, 2, HALF], F32, name="t%d" % e, tag="t%d" % e)
                 prods.append(t)
-            reps = 2 // pieces
+            width = HALF // pieces
+            tabs_v = tabs[:].rearrange("p a r t -> p a (r t)")
             for c in range(pieces):
-                cols = slice(c * 256 * reps, (c + 1) * 256 * reps)
-                for i, e in ((0, 0), (2, 0), (1, 1), (3, 1)):
+                cols = slice(c * width, (c + 1) * width)
+                for e in range(2):
                     nc.vector.scalar_tensor_tensor(
-                        out=prods[i][:, cols].rearrange("p (r t) -> p r t", t=256),
-                        in0=acc[e][:, cols].rearrange("p (r t) -> p r t", t=256),
-                        scalar=bias_of(j, e), in1=table(i, reps), op0=ALU.add, op1=ALU.mult,
+                        out=prods[e][:, :, cols],
+                        in0=acc_of[u][e][:, cols].unsqueeze(1).to_broadcast([P, 2, width]),
+                        scalar=bias_of(j, e),
+                        in1=tabs_v[:, 2 * e : 2 * e + 2, cols],
+                        op0=ALU.add, op1=ALU.mult,
                     )
             prods_of[u] = prods
 
@@ -276,11 +291,11 @@ def tile_gqaselfattention_pa_kernel(
                 cols = slice((2 * b2 + bb) * P, (2 * b2 + bb + 1) * P)
                 for half in range(2):
                     nc.tensor.matmul(
-                        out=bank[:, bb, half, :], lhsT=prods[2 * half][:, cols], rhs=ident[:],
+                        out=bank[:, bb, half, :], lhsT=prods[0][:, half, cols], rhs=ident[:],
                         start=True, stop=False, is_transpose=True,
                     )
                     nc.tensor.matmul(
-                        out=bank[:, bb, half, :], lhsT=prods[2 * half + 1][:, cols], rhs=ident[:],
+                        out=bank[:, bb, half, :], lhsT=prods[1][:, half, cols], rhs=ident[:],
                         start=False, stop=True, is_transpose=True,
                     )
 

@@ -58,7 +58,7 @@ def tile_gqaselfattention_pa_kernel(
         brow_bf = const.tile([P, 256], BF16, name="brow_bf")
         warm = const.tile([P, 1], F32, name="warm")
         warm_out = const.tile([P, 1], F32, name="warm_out")
-        ident = const.tile([P, P], F32, name="ident")
+        ident = const.tile([P, P], F32, name="ident", align_bytes=256)
         ident_bf = const.tile([P, P], BF16, name="ident_bf")
         sc_bc = const.tile([P, K], F32, name="sc_bc")
         sc_k = const.tile([P, PASSES, 4], F32, name="sc_k")
@@ -71,10 +71,10 @@ def tile_gqaselfattention_pa_kernel(
 
         x_sb = []
         for n in range(8):
-            xt = xin.tile([P, K], BF16, name="x_sb", tag="x_sb")
+            xt = xin.tile([P, K], BF16, name="x_sb", tag="x_sb", align_bytes=256)
             x_sb.append(xt)
-        xc = xkeep.tile([P, 2, PASSES, HALF], U32, name="xc", align_bytes=64)
-        xs = xkeep.tile([P, 2, PASSES, HALF], U8, name="xs", align_bytes=64)
+        xc = xkeep.tile([P, 2, PASSES, HALF], U32, name="xc", align_bytes=256)
+        xs = xkeep.tile([P, 2, PASSES, HALF], U8, name="xs", align_bytes=256)
         xg = []
         for h in range(2):
             xgh = xkeep.tile([P, PASSES, HALF, 4], BF16, name="xg%d" % h, align_bytes=64)
@@ -104,7 +104,7 @@ def tile_gqaselfattention_pa_kernel(
         def load_w(n):
             j = order[n]
             if j >= N_Q_PAIRS:
-                wb = wbpool.tile([P, 2, K], BF16, name="wb", tag="wb")
+                wb = wbpool.tile([P, 2, K], BF16, name="wb", tag="wb", align_bytes=256)
                 wb_of[n] = wb
                 nc.sync.dma_start(out=wb[:], in_=wk_view[j - N_Q_PAIRS])
             else:
@@ -116,7 +116,7 @@ def tile_gqaselfattention_pa_kernel(
 
         def widen(n, e, engine):
             if n not in wb_of:
-                wb = wbpool.tile([P, 2, K], BF16, name="wb", tag="wb")
+                wb = wbpool.tile([P, 2, K], BF16, name="wb", tag="wb", align_bytes=256)
                 wb_of[n] = wb
             plain.add(2 * n + e)
             if engine is nc.scalar:
@@ -126,7 +126,7 @@ def tile_gqaselfattention_pa_kernel(
 
         def prod(n, e, lo=0, hi=K):
             if n not in wb_of:
-                wb = wbpool.tile([P, 2, K], BF16, name="wb", tag="wb")
+                wb = wbpool.tile([P, 2, K], BF16, name="wb", tag="wb", align_bytes=256)
                 wb_of[n] = wb
             nc.vector.tensor_tensor(
                 out=wb_of[n][:, e, lo:hi], in0=by_of[n][:, e, lo:hi].bitcast(FP8), in1=sc_bc[:, lo:hi], op=ALU.mult
@@ -208,8 +208,8 @@ def tile_gqaselfattention_pa_kernel(
             transpose_rows(wb_of[n][:, e, :], wg_of[n][:, e, :, :, :], "scaled" if m in plain else ("hold" if hold else (lambda m: ())(m)), where)
 
         def qw(n):
-            wc = wpool.tile([P, 2 * PASSES * P], U32, name="wc", tag="wc", align_bytes=64)
-            ws = wpool.tile([P, 2 * PASSES * P], U8, name="ws", tag="ws", align_bytes=64)
+            wc = wpool.tile([P, 2 * PASSES * P], U32, name="wc", tag="wc", align_bytes=256)
+            ws = wpool.tile([P, 2 * PASSES * P], U8, name="ws", tag="ws", align_bytes=256)
             nc.vector.quantize_mx(
                 out=wc[:].bitcast(FP8X4), scales=ws[:], in_=wg_of[n][:].rearrange("p e g r t -> p (e g r t)")
             )
@@ -267,7 +267,7 @@ def tile_gqaselfattention_pa_kernel(
             j = order[units[u][0]]
             prods = []
             for e in range(2):
-                t = tpool.tile([P, 2, HALF], F32, name="t%d" % e, tag="t%d" % e)
+                t = tpool.tile([P, 2, HALF], F32, name="t%d" % e, tag="t%d" % e, align_bytes=256)
                 prods.append(t)
             width = HALF // pieces
             tabs_v = tabs[:].rearrange("p a r t -> p a (r t)")

@@ -58,7 +58,7 @@ def tile_gqaselfattention_pa_kernel(
         brow_bf = const.tile([P, 256], BF16, name="brow_bf")
         warm = const.tile([P, 1], F32, name="warm")
         warm_out = const.tile([P, 1], F32, name="warm_out")
-        ident = const.tile([P, P], F32, name="ident", align_bytes=256)
+        ident = const.tile([P, P], F32, name="ident")
         ident_bf = const.tile([P, P], BF16, name="ident_bf")
         sc_bc = const.tile([P, K], F32, name="sc_bc")
         sc_k = const.tile([P, PASSES, 4], F32, name="sc_k")
@@ -73,8 +73,8 @@ def tile_gqaselfattention_pa_kernel(
         for n in range(8):
             xt = xin.tile([P, K], BF16, name="x_sb", tag="x_sb", align_bytes=256)
             x_sb.append(xt)
-        xc = xkeep.tile([P, 2, PASSES, HALF], U32, name="xc", align_bytes=256)
-        xs = xkeep.tile([P, 2, PASSES, HALF], U8, name="xs", align_bytes=256)
+        xc = xkeep.tile([P, 2, PASSES, HALF], U32, name="xc", align_bytes=64)
+        xs = xkeep.tile([P, 2, PASSES, HALF], U8, name="xs", align_bytes=64)
         xg = []
         for h in range(2):
             xgh = xkeep.tile([P, PASSES, HALF, 4], BF16, name="xg%d" % h, align_bytes=64)
@@ -98,8 +98,10 @@ def tile_gqaselfattention_pa_kernel(
         rstd_of = {}
         y_of = {}
 
-        def load_x(i):
-            nc.sync.dma_start(out=x_sb[i][:], in_=x_view[i])
+        def load_x(i, pieces=1):
+            for c in range(pieces):
+                cols = slice(c * (K // pieces), (c + 1) * (K // pieces))
+                nc.sync.dma_start(out=x_sb[i][:, cols], in_=x_view[i][:, cols])
 
         def load_w(n):
             j = order[n]
@@ -208,8 +210,8 @@ def tile_gqaselfattention_pa_kernel(
             transpose_rows(wb_of[n][:, e, :], wg_of[n][:, e, :, :, :], "scaled" if m in plain else ("hold" if hold else (lambda m: ())(m)), where)
 
         def qw(n):
-            wc = wpool.tile([P, 2 * PASSES * P], U32, name="wc", tag="wc", align_bytes=256)
-            ws = wpool.tile([P, 2 * PASSES * P], U8, name="ws", tag="ws", align_bytes=256)
+            wc = wpool.tile([P, 2 * PASSES * P], U32, name="wc", tag="wc", align_bytes=64)
+            ws = wpool.tile([P, 2 * PASSES * P], U8, name="ws", tag="ws", align_bytes=64)
             nc.vector.quantize_mx(
                 out=wc[:].bitcast(FP8X4), scales=ws[:], in_=wg_of[n][:].rearrange("p e g r t -> p (e g r t)")
             )
@@ -243,24 +245,28 @@ def tile_gqaselfattention_pa_kernel(
         def bias_of(j, e):
             return bias_sb[:, e, j : j + 1]
 
-        def mx(u):
+        def mx(u, pieces=1):
             n, h = units[u]
             wc, ws = codes_of[n]
             acc = []
             for e in range(2):
                 pe = ps_mx.tile([P, HALF], F32, name="mx", tag="mx")
                 acc.append(pe)
-                for g in range(PASSES):
-                    c = e * PASSES + g
-                    nc.tensor.matmul_mx(
-                        out=pe[:],
-                        lhsT=wc[:, c * P : (c + 1) * P].bitcast(FP8X4),
-                        lhsT_scale=ws[:, c * P : (c + 1) * P],
-                        rhs=xc[:, h, g, :].bitcast(FP8X4),
-                        rhs_scale=xs[:, h, g, :],
-                        start=(g == 0),
-                        stop=(g == PASSES - 1),
-                    )
+            width = HALF // pieces
+            for c in range(pieces):
+                tok = slice(c * width, (c + 1) * width)
+                for e in range(2):
+                    for g in range(PASSES):
+                        col = (e * PASSES + g) * P
+                        nc.tensor.matmul_mx(
+                            out=acc[e][:, tok],
+                            lhsT=wc[:, col : col + P].bitcast(FP8X4),
+                            lhsT_scale=ws[:, col : col + P],
+                            rhs=xc[:, h, g, tok].bitcast(FP8X4),
+                            rhs_scale=xs[:, h, g, tok],
+                            start=(g == 0),
+                            stop=(g == PASSES - 1),
+                        )
             acc_of[u] = acc
 
         def rp(u, pieces=1):
@@ -314,10 +320,10 @@ def tile_gqaselfattention_pa_kernel(
                         accum_out=ss_of[u][:, col : col + 1],
                     )
 
-        def rs(u, b2):
+        def rs(u, b2, lo=0, hi=4):
+            cols = slice(8 * b2 + lo, 8 * b2 + hi)
             nc.scalar.activation(
-                out=rstd_of[u][:, 8 * b2 : 8 * b2 + 4], in_=ss_of[u][:, 8 * b2 : 8 * b2 + 4],
-                func=ACT.Abs_reciprocal_sqrt, bias=EPS, scale=1.0 / 128.0,
+                out=rstd_of[u][:, cols], in_=ss_of[u][:, cols], func=ACT.Abs_reciprocal_sqrt, bias=EPS, scale=1.0 / 128.0,
             )
 
         def rs_unit(u):
@@ -368,21 +374,19 @@ def tile_gqaselfattention_pa_kernel(
                             func=ACT.Copy,
                             scale=rstd[:, col : col + 1],
                         )
-            if pieces[-1] != 3:
+            if pieces[-1] != 3 and not on_vector:
                 return
             if not on_vector:
                 yb = y[:, 2 * b2 : 2 * b2 + 2, :, :].rearrange("p b h d -> p (b h) d")
                 nc.gpsimd.tensor_tensor(
                     out=yb, in0=yb, in1=gain[:].unsqueeze(1).to_broadcast([P, 4, P]), op=ALU.mult
                 )
-            nc.sync.dma_start(
-                out=dst[:, 2 * b2 : 2 * b2 + 2, :],
-                in_=y[:, 2 * b2 : 2 * b2 + 2, :, :].rearrange("p b h d -> p b (h d)"),
-            )
+            blocks = slice(2 * b2 + (pieces[0] // 2 if on_vector else 0), 2 * b2 + pieces[-1] // 2 + 1)
+            nc.sync.dma_start(out=dst[:, blocks, :], in_=y[:, blocks, :, :].rearrange("p b h d -> p b (h d)"))
 
-        for kind, i in (("w", 0), ("s", 0), ("s", 1), ("b", 0), ("x", 0), ("x", 1), ("x", 2), ("x", 3), ("w", 1), ("x", 4), ("x", 5), ("x", 6), ("x", 7), ("w", 2), ("w", 3), ("w", 4), ("g", 0)):
+        for kind, i in (("w", 0), ("s", 0), ("x", 0), ("s", 1), ("x", 1), ("w", 1), ("x", 2), ("x", 3), ("b", 0), ("x", 4), ("x", 5), ("x", 6), ("x", 7), ("w", 2), ("w", 3), ("w", 4), ("g", 0)):
             if kind == "x":
-                load_x(i)
+                load_x(i, 1 if i == 0 else 1)
             elif kind == "w":
                 load_w(i)
             elif kind == "s":
@@ -390,8 +394,6 @@ def tile_gqaselfattention_pa_kernel(
                     out=sc_bc[:, i * 1024 : (i + 1) * 1024],
                     in_=Wq_scale.rearrange("o k -> (o k)")[i * 1024 : (i + 1) * 1024].partition_broadcast(P),
                 )
-            elif kind == "k":
-                nc.sync.dma_start(out=sc_k[:], in_=Wq_scale.rearrange("o (g p t) -> p (o g) t", p=P, t=4))
             elif kind == "b":
                 nc.sync.dma_start(out=brow_bf[0:N_Q_PAIRS, :], in_=bq.rearrange("(j c) -> j c", c=256))
                 nc.sync.dma_start(out=brow_bf[N_Q_PAIRS:N_PAIRS, :], in_=bk.rearrange("(j c) -> j c", c=256))
@@ -425,49 +427,48 @@ def tile_gqaselfattention_pa_kernel(
             if e == 1:
                 more_loads()
 
-        shared = lambda u: False
         setup_tables()
         for c in range(2):
             for e in range(2):
                 prod(0, e, c * 1024, (c + 1) * 1024)
         state["p"] = 2
         more_loads()
-        xt_(0, ("mx", "mx"))
-        xt_(1, ("mx", "mx"))
-        qx(0, 0)
-        bt(0, ("mx", "mx"))
-        xt_(2, ("mx", "mx"))
-        bt(1, ("mx", "mx"))
-        xt_(3, ("mx", "mx"))
         next_prod(1)
+        xt_(0, ("tp", "ot"))
+        bt(0, ("tp", "tp"))
+        xt_(1, ("tp", "ot"))
+        bt(1, ("tp", "ot"))
+        xt_(2, ("mx", "mx"))
+        qx(0, 0)
         qw(0)
+        xt_(3, ("mx", "mx"))
         qx(0, 1)
-        xt_(4, ("tp", "ot"))
-        xt_(5, ("tp", "ot"))
+        next_prod(1)
+        xt_(4, ("ot", "ot"))
+        bt(2, ("mx", "mx"))
+        xt_(5, ("tp", "tp"))
         setup_bias()
         mx(0)
-        next_prod(1)
-        bt(2, ("tp", "ot"))
-        qx(1, 0)
-        xt_(6, ("tp", "ot"))
-        xt_(7, ("tp", "ot"))
-        bt(3, ("tp", "ot"))
         rp(0)
-        qx(1, 1)
-        mx(1)
-        qw(1)
+        qx(1, 0)
         next_prod(1)
-        rp(1)
+        xt_(6, ("ot", "ot"))
+        xt_(7, ("mx", "mx"))
+        bt(3, ("mx", "mx"))
+        bt(4, ("tp", "tp"))
         ot(0, 0)
         ot(0, 1)
         sq(0, 0)
         rs(0, 0)
         sq(0, 1)
-        bt(4, ("tp", "tp"))
+        qx(1, 1)
+        mx(1)
+        qw(1)
+        rp(1)
         for k in range(1, N_UNITS):
             by_vector = k - 1 >= N_UNITS - 2
             if k + 1 < N_UNITS:
-                mx(k + 1)
+                mx(k + 1, 2 if k + 1 == N_UNITS - 1 else 1)
             if due(k) or k % 2 == 1:
                 next_prod()
             if not by_vector:
@@ -500,8 +501,9 @@ def tile_gqaselfattention_pa_kernel(
             else:
                 for b2 in range(2):
                     ot(k, b2, where)
-                    sq(k, b2)
-                    rs(k, b2)
-                    finish(k, b2, True)
+                    for piece in ((0, 1), (2, 3)) if b2 == 1 else ((0, 1, 2, 3),):
+                        sq(k, b2, piece)
+                        rs(k, b2, piece[0], piece[-1] + 1)
+                        finish(k, b2, True, piece)
             if (k + 3) % 2 == 0 and (k + 3) // 2 < N_PAIRS:
                 qw((k + 3) // 2)

@@ -468,7 +468,7 @@ def tile_gqaselfattention_pa_kernel(
         for k in range(1, N_UNITS):
             by_vector = k - 1 >= N_UNITS - 2
             if k + 1 < N_UNITS:
-                mx(k + 1, 2 if k + 1 == N_UNITS - 1 else 1)
+                mx(k + 1)
             if due(k) or k % 2 == 1:
                 next_prod()
             if not by_vector:
@@ -501,9 +501,8 @@ def tile_gqaselfattention_pa_kernel(
             else:
                 for b2 in range(2):
                     ot(k, b2, where)
-                    for piece in ((0, 1), (2, 3)) if b2 == 1 else ((0, 1, 2, 3),):
-                        sq(k, b2, piece)
-                        rs(k, b2, piece[0], piece[-1] + 1)
-                        finish(k, b2, True, piece)
+                    sq(k, b2)
+                    rs(k, b2)
+                    finish(k, b2, True)
             if (k + 3) % 2 == 0 and (k + 3) // 2 < N_PAIRS:
                 qw((k + 3) // 2)

from contextlib import ExitStack

import concourse.mybir as mybir
from concourse.masks import make_identity

F32 = mybir.dt.float32
BF16 = mybir.dt.bfloat16
U32 = mybir.dt.uint32
U8 = mybir.dt.uint8
FP8 = mybir.dt.float8_e4m3fn
FP8X4 = mybir.dt.float8_e4m3fn_x4
ALU = mybir.AluOpType
ACT = mybir.ActivationFunctionType

P = 128
K = 2048
PASSES = 4
TOKENS = 1024
HALF = 512
EPS = 1e-6
N_Q_PAIRS = 8
N_K_PAIRS = 2
N_PAIRS = N_Q_PAIRS + N_K_PAIRS
N_UNITS = 2 * N_PAIRS
V_TAIL = 2

FLOPS = 2 * TOKENS * (2048 + 512) * K


def tile_gqaselfattention_pa_kernel(
    tc, x, Wq_bytes, Wq_scale, bq, Wk, bk, qn_w, kn_w, cos, sin, out_0, out_1
):
    nc = tc.nc
    x_view = x.flatten_outer_dims().rearrange("(n p) k -> n p k", p=P)
    wq_view = Wq_bytes.rearrange("(j p e) k -> j p e k", p=P, e=2)
    wk_view = Wk.rearrange("(j p e) k -> j p e k", p=P, e=2)
    oq_view = out_0.rearrange("b t h d -> (b t) (h d)").rearrange("(n p) c -> p n c", p=P)
    ok_view = out_1.rearrange("b t h d -> (b t) (h d)").rearrange("(n p) c -> p n c", p=P)
    order = [0, 1, 8, 2, 3, 4, 9, 5, 6, 7]
    units = [(n, h) for n in range(N_PAIRS) for h in range(2)]

    with ExitStack() as ctx:
        const = ctx.enter_context(tc.tile_pool(name="const", bufs=1))
        xin = ctx.enter_context(tc.tile_pool(name="xin", bufs=8))
        xkeep = ctx.enter_context(tc.tile_pool(name="xkeep", bufs=1))
        bpool = ctx.enter_context(tc.tile_pool(name="bpool", bufs=4))
        wbpool = ctx.enter_context(tc.tile_pool(name="wbpool", bufs=5))
        wpool = ctx.enter_context(tc.tile_pool(name="wpool", bufs=3))
        gpool = ctx.enter_context(tc.tile_pool(name="gpool", bufs=2))
        tpool = ctx.enter_context(tc.tile_pool(name="tpool", bufs=2))
        ypool = ctx.enter_context(tc.tile_pool(name="ypool", bufs=3))
        spool = ctx.enter_context(tc.tile_pool(name="spool", bufs=4))
        ps_tp = ctx.enter_context(tc.psum_pool(name="ps_tp", bufs=2))
        ps_mx = ctx.enter_context(tc.psum_pool(name="ps_mx", bufs=4))
        ps_ot = ctx.enter_context(tc.psum_pool(name="ps_ot", bufs=2))

        cs_bf = const.tile([P, 2, 2, 2, 64], BF16, name="cs_bf")
        brow_bf = const.tile([P, 256], BF16, name="brow_bf")
        warm = const.tile([P, 1], F32, name="warm")
        warm_out = const.tile([P, 1], F32, name="warm_out")
        ident = const.tile([P, P], F32, name="ident")
        ident_bf = const.tile([P, P], BF16, name="ident_bf")
        sc_bc = const.tile([P, K], F32, name="sc_bc")
        sc_k = const.tile([P, PASSES, 4], F32, name="sc_k")
        wq_bc = const.tile([P, P], BF16, name="wq_bc")
        wk_bc = const.tile([P, P], BF16, name="wk_bc")
        nc.vector.memset(brow_bf[:], 0.0)
        nc.vector.memset(warm[:], 1.0)
        make_identity(nc, ident_bf[:])
        make_identity(nc, ident[:])

        x_sb = []
        for n in range(8):
            xt = xin.tile([P, K], BF16, name="x_sb", tag="x_sb", align_bytes=256)
            x_sb.append(xt)
        xc = xkeep.tile([P, 2, PASSES, HALF], U32, name="xc", align_bytes=64)
        xs = xkeep.tile([P, 2, PASSES, HALF], U8, name="xs", align_bytes=64)
        xg = []
        for h in range(2):
            xgh = xkeep.tile([P, PASSES, HALF, 4], BF16, name="xg%d" % h, align_bytes=64)
            xg.append(xgh)

        ctx.enter_context(tc.manual_schedule())

        for c, src in ((0, cos), (1, sin)):
            for hh in range(2):
                nc.sync.dma_start(out=cs_bf[:, c, :, hh, :], in_=src.rearrange("(b p) i -> p b i", p=P))
        nc.scalar.activation(out=warm_out[:], in_=warm[:], func=ACT.Abs_reciprocal_sqrt)

        wb_of = {}
        by_of = {}
        wg_of = {}
        codes_of = {}
        acc_of = {}
        prods_of = {}
        ots_of = {}
        ss_of = {}
        rstd_of = {}
        y_of = {}

        def load_x(i, pieces=1):
            for c in range(pieces):
                cols = slice(c * (K // pieces), (c + 1) * (K // pieces))
                nc.sync.dma_start(out=x_sb[i][:, cols], in_=x_view[i][:, cols])

        def load_w(n):
            j = order[n]
            if j >= N_Q_PAIRS:
                wb = wbpool.tile([P, 2, K], BF16, name="wb", tag="wb", align_bytes=256)
                wb_of[n] = wb
                nc.sync.dma_start(out=wb[:], in_=wk_view[j - N_Q_PAIRS])
            else:
                by = bpool.tile([P, 2, K], U8, name="wq_bytes_sb", tag="wq_bytes_sb")
                by_of[n] = by
                nc.sync.dma_start(out=by[:], in_=wq_view[j])

        plain = set()

        def widen(n, e, engine):
            if n not in wb_of:
                wb = wbpool.tile([P, 2, K], BF16, name="wb", tag="wb", align_bytes=256)
                wb_of[n] = wb
            plain.add(2 * n + e)
            if engine is nc.scalar:
                nc.scalar.copy(out=wb_of[n][:, e, :], in_=by_of[n][:, e, :].bitcast(FP8))
            else:
                engine.tensor_copy(out=wb_of[n][:, e, :], in_=by_of[n][:, e, :].bitcast(FP8))

        def prod(n, e, lo=0, hi=K):
            if n not in wb_of:
                wb = wbpool.tile([P, 2, K], BF16, name="wb", tag="wb", align_bytes=256)
                wb_of[n] = wb
            nc.vector.tensor_tensor(
                out=wb_of[n][:, e, lo:hi], in0=by_of[n][:, e, lo:hi].bitcast(FP8), in1=sc_bc[:, lo:hi], op=ALU.mult
            )

        def head_bank(where):
            if where == "mx":
                bank = ps_mx.tile([P, 2, 2, P], F32, name="mx", tag="mx")
            elif where == "ot":
                bank = ps_ot.tile([P, 2, 2, P], F32, name="ot", tag="ot")
            else:
                bank = ps_tp.tile([P, 2, 2, P], F32, name="tp", tag="tp")
            return bank

        def scaled_exit(tp, dst, gp):
            nc.vector.tensor_tensor(
                out=dst.rearrange("p g r (u e) -> p g r u e", e=2),
                in0=tp[:].bitcast(BF16).rearrange("p u g (r e) -> p g r u e", e=2),
                in1=sc_k[:, 2 * gp : 2 * gp + 2, :]
                .rearrange("p g (u e) -> p g u e", e=2)
                .unsqueeze(2)
                .to_broadcast([P, 2, P, 2, 2]),
                op=ALU.mult,
            )

        held = []

        def flush(c=2):
            for i in range(min(c, len(held))):
                tp, dst = held.pop(0)
                nc.scalar.copy(out=dst, in_=tp[:].rearrange("p u g r -> p g r u"))

        def transpose_rows(src_bf, dst, vx, where=("tp", "tp")):
            words = src_bf.bitcast(F32)
            for gp in range(2):
                tp = head_bank(where[gp])
                for g2 in range(2):
                    g = 2 * gp + g2
                    for u in range(2):
                        nc.tensor.transpose(
                            tp[:, u, g2, :], words[:, 256 * g + u : 256 * (g + 1) : 2], ident[:]
                        )
                if vx == "scaled":
                    scaled_exit(tp, dst[:, 2 * gp : 2 * gp + 2, :, :], gp)
                    continue
                if vx == "hold":
                    held.append((tp, dst.bitcast(F32)[:, 2 * gp : 2 * gp + 2, :, :]))
                    continue
                (nc.vector.tensor_copy if gp in vx else nc.scalar.copy)(
                    out=dst.bitcast(F32)[:, 2 * gp : 2 * gp + 2, :, :],
                    in_=tp[:].rearrange("p u g r -> p g r u"),
                )

        def xt_(i, where):
            h, tl = divmod(i, 4)
            transpose_rows(x_sb[i][:], xg[h][:, :, tl * P : (tl + 1) * P, :], (lambda i: ())(i), where)

        def qx(h, tp2):
            cols = slice(tp2 * 256, (tp2 + 1) * 256)
            for g in range(PASSES):
                nc.vector.quantize_mx(
                    out=xc[:, h, g, cols].bitcast(FP8X4),
                    scales=xs[:, h, g, cols],
                    in_=xg[h][:, g, cols, :].rearrange("p n t -> p (n t)"),
                )

        def qx_wide(h, gp):
            nc.vector.quantize_mx(
                out=xc[:, h, 2 * gp : 2 * gp + 2, :].rearrange("p g n -> p (g n)").bitcast(FP8X4),
                scales=xs[:, h, 2 * gp : 2 * gp + 2, :].rearrange("p g n -> p (g n)"),
                in_=xg[h][:, 2 * gp : 2 * gp + 2, :, :].rearrange("p g n t -> p (g n t)"),
            )

        def bt(m, where=("tp", "tp"), hold=False):
            n, e = divmod(m, 2)
            if e == 0:
                wg = gpool.tile([P, 2, PASSES, P, 4], BF16, name="wg", tag="wg", align_bytes=64)
                wg_of[n] = wg
            transpose_rows(wb_of[n][:, e, :], wg_of[n][:, e, :, :, :], "scaled" if m in plain else ("hold" if hold else (lambda m: ())(m)), where)

        def qw(n):
            wc = wpool.tile([P, 2 * PASSES * P], U32, name="wc", tag="wc", align_bytes=64)
            ws = wpool.tile([P, 2 * PASSES * P], U8, name="ws", tag="ws", align_bytes=64)
            nc.vector.quantize_mx(
                out=wc[:].bitcast(FP8X4), scales=ws[:], in_=wg_of[n][:].rearrange("p e g r t -> p (e g r t)")
            )
            codes_of[n] = (wc, ws)

        tabs = const.tile([P, 4, 2, 256], F32, name="tabs")

        def setup_tables():
            tp_cs = ps_ot.tile([P, 2, 2, P], BF16, name="ot", tag="ot")
            for c in range(2):
                for b in range(2):
                    nc.tensor.transpose(
                        tp_cs[:, c, b, :], cs_bf[:, c, b, :, :].rearrange("p h i -> p (h i)"), ident_bf[:]
                    )
            cs_t = tp_cs[:].rearrange("p c b t -> p c (b t)")
            for r in range(2):
                nc.vector.tensor_copy(out=tabs[:, 0:2, r, :], in_=cs_t)
            for r in range(2):
                nc.scalar.mul(out=tabs[:, 2, r, :], in_=cs_t[:, 1, :], mul=-1.0)
            nc.vector.tensor_copy(out=tabs[:, 3, :, :], in_=tabs[:, 0, :, :])

        bias_sb = const.tile([P, 2, N_PAIRS], F32, name="bias_sb")

        def setup_bias():
            tp_b = ps_ot.tile([P, 2, P], BF16, name="ot", tag="ot")
            brow_v = brow_bf[:].rearrange("p (c e) -> p e c", e=2)
            for e in range(2):
                nc.tensor.transpose(tp_b[:, e, :], brow_v[:, e, :], ident_bf[:])
            nc.vector.tensor_copy(out=bias_sb[:], in_=tp_b[:, :, 0:N_PAIRS])

        def bias_of(j, e):
            return bias_sb[:, e, j : j + 1]

        def mx(u, pieces=1):
            n, h = units[u]
            wc, ws = codes_of[n]
            acc = []
            for e in range(2):
                pe = ps_mx.tile([P, HALF], F32, name="mx", tag="mx")
                acc.append(pe)
            width = HALF // pieces
            for c in range(pieces):
                tok = slice(c * width, (c + 1) * width)
                for e in range(2):
                    for g in range(PASSES):
                        col = (e * PASSES + g) * P
                        nc.tensor.matmul_mx(
                            out=acc[e][:, tok],
                            lhsT=wc[:, col : col + P].bitcast(FP8X4),
                            lhsT_scale=ws[:, col : col + P],
                            rhs=xc[:, h, g, tok].bitcast(FP8X4),
                            rhs_scale=xs[:, h, g, tok],
                            start=(g == 0),
                            stop=(g == PASSES - 1),
                        )
            acc_of[u] = acc

        def rp(u, pieces=1):
            j = order[units[u][0]]
            prods = []
            for e in range(2):
                t = tpool.tile([P, 2, HALF], F32, name="t%d" % e, tag="t%d" % e, align_bytes=256)
                prods.append(t)
            width = HALF // pieces
            tabs_v = tabs[:].rearrange("p a r t -> p a (r t)")
            for c in range(pieces):
                cols = slice(c * width, (c + 1) * width)
                for e in range(2):
                    nc.vector.scalar_tensor_tensor(
                        out=prods[e][:, :, cols],
                        in0=acc_of[u][e][:, cols].unsqueeze(1).to_broadcast([P, 2, width]),
                        scalar=bias_of(j, e),
                        in1=tabs_v[:, 2 * e : 2 * e + 2, cols],
                        op0=ALU.add, op1=ALU.mult,
                    )
            prods_of[u] = prods

        def ot(u, b2, where="ot"):
            prods = prods_of[u]
            bank = head_bank(where)
            ots_of.setdefault(u, []).append(bank)
            for bb in range(2):
                cols = slice((2 * b2 + bb) * P, (2 * b2 + bb + 1) * P)
                for half in range(2):
                    nc.tensor.matmul(
                        out=bank[:, bb, half, :], lhsT=prods[0][:, half, cols], rhs=ident[:],
                        start=True, stop=False, is_transpose=True,
                    )
                    nc.tensor.matmul(
                        out=bank[:, bb, half, :], lhsT=prods[1][:, half, cols], rhs=ident[:],
                        start=False, stop=True, is_transpose=True,
                    )

        def sq(u, b2, pieces=(0, 1, 2, 3)):
            if b2 == 0 and pieces[0] == 0:
                ss = spool.tile([P, 16], F32, name="ss", tag="ss")
                ss_of[u] = ss
                rstd = spool.tile([P, 16], F32, name="rstd", tag="rstd")
                rstd_of[u] = rstd
            for i in pieces:
                    bb, hh = divmod(i, 2)
                    col = 8 * b2 + 2 * bb + hh
                    junk = spool.tile([P, 2, 64], F32, name="junk", tag="junk")
                    nc.scalar.activation(
                        out=junk[:], in_=ots_of[u][b2][:, bb, :, hh * 64 : (hh + 1) * 64], func=ACT.Square,
                        accum_out=ss_of[u][:, col : col + 1],
                    )

        def rs(u, b2, lo=0, hi=4):
            cols = slice(8 * b2 + lo, 8 * b2 + hi)
            nc.scalar.activation(
                out=rstd_of[u][:, cols], in_=ss_of[u][:, cols], func=ACT.Abs_reciprocal_sqrt, bias=EPS, scale=1.0 / 128.0,
            )

        def rs_unit(u):
            nc.scalar.activation(
                out=rstd_of[u][:].rearrange("p (b c) -> p b c", b=2)[:, :, 0:4],
                in_=ss_of[u][:].rearrange("p (b c) -> p b c", b=2)[:, :, 0:4],
                func=ACT.Abs_reciprocal_sqrt, bias=EPS, scale=1.0 / 128.0,
            )

        def ot_sq(u):
            ot(u, 0)
            ot(u, 1)
            sq(u, 0)
            sq(u, 1)
            rs_unit(u)

        def finish(u, b2, on_vector, pieces=(0, 1, 2, 3)):
            n, h = units[u]
            j = order[n]
            bank = ots_of[u][b2]
            rstd = rstd_of[u]
            gain = wq_bc if j < N_Q_PAIRS else wk_bc
            if j < N_Q_PAIRS:
                dst = oq_view[:, 4 * h : 4 * h + 4, 256 * j : 256 * (j + 1)]
            else:
                dst = ok_view[:, 4 * h : 4 * h + 4, 256 * (j - N_Q_PAIRS) : 256 * (j - N_Q_PAIRS + 1)]
            if b2 == 0 and pieces[0] == 0:
                y = ypool.tile([P, 4, 2, P], F32, name="y", tag="y")
                y_of[u] = y
            y = y_of[u]
            for i in pieces:
                    bb, hh = divmod(i, 2)
                    blk = 2 * b2 + bb
                    col = 8 * b2 + 2 * bb + hh
                    if on_vector:
                        nc.vector.scalar_tensor_tensor(
                            out=y[:, blk, hh, :].rearrange("p (a i) -> p a i", a=2),
                            in0=bank[:, bb, :, hh * 64 : (hh + 1) * 64],
                            scalar=rstd[:, col : col + 1],
                            in1=gain[:].rearrange("p (a i) -> p a i", a=2),
                            op0=ALU.mult,
                            op1=ALU.mult,
                        )
                    else:
                        nc.scalar.activation(
                            out=y[:, blk, hh, :].rearrange("p (a i) -> p a i", a=2),
                            in_=bank[:, bb, :, hh * 64 : (hh + 1) * 64],
                            func=ACT.Copy,
                            scale=rstd[:, col : col + 1],
                        )
            if pieces[-1] != 3 and not on_vector:
                return
            if not on_vector:
                yb = y[:, 2 * b2 : 2 * b2 + 2, :, :].rearrange("p b h d -> p (b h) d")
                nc.gpsimd.tensor_tensor(
                    out=yb, in0=yb, in1=gain[:].unsqueeze(1).to_broadcast([P, 4, P]), op=ALU.mult
                )
            blocks = slice(2 * b2 + (pieces[0] // 2 if on_vector else 0), 2 * b2 + pieces[-1] // 2 + 1)
            nc.sync.dma_start(out=dst[:, blocks, :], in_=y[:, blocks, :, :].rearrange("p b h d -> p b (h d)"))

        for kind, i in (("w", 0), ("s", 0), ("x", 0), ("s", 1), ("x", 1), ("w", 1), ("x", 2), ("x", 3), ("b", 0), ("x", 4), ("x", 5), ("x", 6), ("x", 7), ("w", 2), ("w", 3), ("w", 4), ("g", 0)):
            if kind == "x":
                load_x(i, 1 if i == 0 else 1)
            elif kind == "w":
                load_w(i)
            elif kind == "s":
                nc.sync.dma_start(
                    out=sc_bc[:, i * 1024 : (i + 1) * 1024],
                    in_=Wq_scale.rearrange("o k -> (o k)")[i * 1024 : (i + 1) * 1024].partition_broadcast(P),
                )
            elif kind == "b":
                nc.sync.dma_start(out=brow_bf[0:N_Q_PAIRS, :], in_=bq.rearrange("(j c) -> j c", c=256))
                nc.sync.dma_start(out=brow_bf[N_Q_PAIRS:N_PAIRS, :], in_=bk.rearrange("(j c) -> j c", c=256))
            else:
                nc.sync.dma_start(out=wq_bc[:], in_=qn_w.partition_broadcast(P))
                nc.sync.dma_start(out=wk_bc[:], in_=kn_w.partition_broadcast(P))
        state = {"p": 0, "l": 5}
        qhalves = [2 * n + e for n in range(N_PAIRS) for e in range(2) if order[n] < N_Q_PAIRS]

        def more_loads():
            if state["l"] < N_PAIRS:
                load_w(state["l"])
                state["l"] += 1

        def next_prod(c=1):
            for i in range(c):
                if state["p"] < len(qhalves):
                    n, e = divmod(qhalves[state["p"]], 2)
                    prod(n, e)
                    state["p"] += 1
                    if e == 1:
                        more_loads()

        def due(k):
            return state["p"] < len(qhalves) and qhalves[state["p"]] <= k + 5

        def next_widen(engine):
            n, e = divmod(qhalves[state["p"]], 2)
            widen(n, e, engine)
            state["p"] += 1
            if e == 1:
                more_loads()

        setup_tables()
        for c in range(2):
            for e in range(2):
                prod(0, e, c * 1024, (c + 1) * 1024)
        state["p"] = 2
        more_loads()
        next_prod(1)
        xt_(0, ("tp", "ot"))
        bt(0, ("tp", "tp"))
        xt_(1, ("tp", "ot"))
        bt(1, ("tp", "ot"))
        xt_(2, ("mx", "mx"))
        qx(0, 0)
        qw(0)
        xt_(3, ("mx", "mx"))
        qx(0, 1)
        next_prod(1)
        xt_(4, ("ot", "ot"))
        bt(2, ("mx", "mx"))
        xt_(5, ("tp", "tp"))
        setup_bias()
        mx(0)
        rp(0)
        qx(1, 0)
        next_prod(1)
        xt_(6, ("ot", "ot"))
        xt_(7, ("mx", "mx"))
        bt(3, ("mx", "mx"))
        bt(4, ("tp", "tp"))
        ot(0, 0)
        ot(0, 1)
        sq(0, 0)
        rs(0, 0)
        sq(0, 1)
        qx(1, 1)
        mx(1)
        qw(1)
        rp(1)
        for k in range(1, N_UNITS):
            by_vector = k - 1 >= N_UNITS - 2
            if k + 1 < N_UNITS:
                mx(k + 1)
            if due(k) or k % 2 == 1:
                next_prod()
            if not by_vector:
                finish(k - 1, 0, False, (0, 1))
                rs(k - 1, 1)
                finish(k - 1, 0, False, (2, 3))
                finish(k - 1, 1, False)
            m = k + 4
            if m < 2 * N_PAIRS:
                if order[m // 2] >= N_Q_PAIRS and m % 2 == 1:
                    more_loads()
                bt(m)
            if k + 1 < N_UNITS:
                rp(k + 1, 2 if k + 1 == N_UNITS - 1 else 1)
            if by_vector:
                finish(k - 1, 0, True)
                finish(k - 1, 1, True)
            where = "tp" if (k >= N_UNITS - 4 and k % 2 == 1) else "ot"
            if k < N_UNITS - 1:
                ot(k, 0, where)
                ot(k, 1, where)
                sq(k, 0)
                if k < N_UNITS - 2:
                    sq(k, 1, (0, 1))
                    rs(k, 0)
                    sq(k, 1, (2, 3))
                else:
                    sq(k, 1)
                    rs_unit(k)
            else:
                for b2 in range(2):
                    ot(k, b2, where)
                    sq(k, b2)
                    rs(k, b2)
                    finish(k, b2, True)
            if (k + 3) % 2 == 0 and (k + 3) // 2 < N_PAIRS:
                qw((k + 3) // 2)
